import numpy as np
import ml_dtypes


def mxq(x, axis, fmt="e4m3"):
    dtype, down = {"e4m3": (ml_dtypes.float8_e4m3fn, 7), "e5m2": (ml_dtypes.float8_e5m2, 14)}[fmt]
    v = np.moveaxis(np.asarray(x, np.float32).astype(ml_dtypes.bfloat16).astype(np.float64), axis, -1)
    blocks = v.reshape(v.shape[:-1] + (-1, 32))
    amax = np.abs(blocks).max(-1, keepdims=True)
    byte = np.maximum(np.where(amax > 0, np.frexp(amax)[1] - 1 + 127, 0) - down, 1)
    scale = np.exp2(byte - 127.0)
    codes = (blocks / scale).astype(np.float32).astype(dtype).astype(np.float64)
    return np.moveaxis((codes * scale).reshape(v.shape), -1, axis)


WIDE = False


def mx_kscale(k):
    if not WIDE:
        return np.ones(k)
    levels = np.array([10, -10, 5, -5, 0])
    a = np.random.permutation(np.resize(levels, k // 512 * 4)).reshape(k // 512, 4)
    idx = np.arange(k)
    return np.exp2(a[idx // 512, idx % 128 // 32])


BF16 = ml_dtypes.bfloat16


def bf(x):
    return np.asarray(x, np.float32).astype(BF16)


def f64(x):
    return np.asarray(x).astype(np.float64)


E2M1 = np.array([0.0, 0.5, 1.0, 1.5, 2.0, 3.0, 4.0, 6.0, -0.0, -0.5, -1.0, -1.5, -2.0, -3.0, -4.0, -6.0])


def pack_weight(w, fmt):
    k, n = w.shape
    w = f64(bf(w)).reshape(k // 32, 32, n)
    amax = np.abs(w).max(1)
    if fmt == "e4m3":
        byte = np.frexp(amax)[1] - 1 + 127 - 7
    else:
        mant, ex = np.frexp(amax / 6.0)
        byte = np.where(mant > 0.5, ex, ex - 1) + 127
    byte = np.clip(np.where(amax > 0, byte, 1), 1, 254)
    scaled = (w * np.exp2(127.0 - byte)[:, None, :]).reshape(k, n).astype(np.float32)
    by_word = np.ascontiguousarray(scaled.reshape(k // 512, 128, 4, n).transpose(0, 1, 3, 2))
    if fmt == "e4m3":
        words = by_word.astype(ml_dtypes.float8_e4m3fn).view(np.uint8)
    else:
        c = by_word.astype(ml_dtypes.float4_e2m1fn).view(np.uint8) & 0xF
        words = c[..., 0::2] | (c[..., 1::2] << 4)
    return np.ascontiguousarray(words), np.ascontiguousarray(byte.astype(np.uint8).reshape(k // 512, 16, n))


def unpack_weight(words, scales, fmt):
    g, p, n, _ = words.shape
    if fmt == "e4m3":
        vals = np.ascontiguousarray(words).view(ml_dtypes.float8_e4m3fn).astype(np.float64)
    else:
        nib = np.empty((g, p, n, 4), np.uint8)
        nib[..., 0::2] = words & 0xF
        nib[..., 1::2] = words >> 4
        vals = E2M1[nib]
    vals = vals * np.repeat(np.exp2(scales.astype(np.float64) - 127.0), 8, axis=1)[..., None]
    return vals.transpose(0, 1, 3, 2).reshape(g * 512, n)

def pack4(w):
    words, scales = pack_weight(w, "e2m1")
    return words.reshape(words.shape[0], 128, -1), scales


def unpack4(words, scales):
    return unpack_weight(words.reshape(words.shape[0], 128, -1, 2), scales, "e2m1")


B, S, D = 128, 16, 512


def sigmoid(v):
    return 1.0 / (1.0 + np.exp(-v))


def setup_inputs():
    s, t = mx_kscale(D), mx_kscale(D)
    inputs = bf(np.random.standard_normal((B, D)) * s)
    h_state = bf((np.random.standard_normal((B, S, D)) * 0.5 * t).reshape(B, S * D))
    c_state = bf(np.random.standard_normal((B, S * D)) * 0.5)
    c_upd = bf(np.random.standard_normal((B, S, D)))
    kernel_words, kernel_scales = pack4(np.random.standard_normal((D, 3 * D)) / np.sqrt(D) / s[:, None])
    recurrent_kernel_words, recurrent_kernel_scales = pack4(np.random.standard_normal((D, 3 * D)) / np.sqrt(D) / t[:, None])
    bias = bf(np.random.standard_normal(3 * D) * 0.3)
    return {
        "inputs": inputs,
        "h_state": h_state,
        "c_state": c_state,
        "c_upd": c_upd,
        "kernel_words": kernel_words,
        "kernel_scales": kernel_scales,
        "recurrent_kernel_words": recurrent_kernel_words,
        "recurrent_kernel_scales": recurrent_kernel_scales,
        "bias": bias,
    }


def reference(inputs, h_state, c_state, c_upd, kernel_words, kernel_scales, recurrent_kernel_words, recurrent_kernel_scales, bias):
    h_tm1 = f64(h_state).reshape(B, S, D)
    c_tm1 = f64(c_state).reshape(B, S, D)
    xz = mxq(f64(inputs), 1, "e4m3") @ unpack4(kernel_words, kernel_scales)
    hz = mxq(h_tm1, 2, "e4m3") @ unpack4(recurrent_kernel_words, recurrent_kernel_scales)
    z = xz[:, None, :] + hz + f64(bias)
    i = sigmoid(z[..., :D])
    f = sigmoid(z[..., D:2 * D])
    o = sigmoid(z[..., 2 * D:])
    c_new = f * c_tm1 + i * np.tanh(f64(c_upd))
    h_new = o * np.tanh(c_new)
    return h_new.reshape(B, -1), c_new.reshape(B, -1)

@@ -1,0 +1,230 @@
+from contextlib import ExitStack
+
+import concourse.mybir as mybir
+from concourse.masks import make_identity
+
+FP32 = mybir.dt.float32
+BF16 = mybir.dt.bfloat16
+I32 = mybir.dt.int32
+U32 = mybir.dt.uint32
+U8 = mybir.dt.uint8
+E4M3X4 = mybir.dt.float8_e4m3fn_x4
+E2M1X4 = mybir.dt.float4_e2m1fn_x4
+SIGMOID = mybir.ActivationFunctionType.Sigmoid
+TANH = mybir.ActivationFunctionType.Tanh
+MULT = mybir.AluOpType.mult
+ADD = mybir.AluOpType.add
+
+P = 128
+SLOTS = 16
+WIDTH = 512
+GATE_I, GATE_F, GATE_O = 0, 1, 2
+CHUNKS = WIDTH // P
+GROUP_SLOTS = 4
+N_GROUPS = SLOTS // GROUP_SLOTS
+GROUP_COLS = GROUP_SLOTS * WIDTH
+PASS_COLS = GROUP_SLOTS * P
+WORDS = WIDTH // 2
+W_X, W_H = 0, 1
+O_LAG = 1
+
+FLOPS = 2 * WIDTH * 3 * WIDTH * (P + P * SLOTS)
+
+
+def tile_rlstmcell_pb_kernel(
+    tc,
+    inputs,
+    h_state,
+    c_state,
+    c_upd,
+    kernel_words,
+    kernel_scales,
+    recurrent_kernel_words,
+    recurrent_kernel_scales,
+    bias,
+    out_0,
+    out_1,
+):
+    nc = tc.nc
+    c_upd_rows = c_upd.rearrange("b s d -> b (s d)")
+
+    with ExitStack() as ctx:
+        ctx.enter_context(tc.manual_schedule())
+        consts = ctx.enter_context(tc.tile_pool(name="consts", bufs=1))
+        loads = ctx.enter_context(tc.tile_pool(name="loads", bufs=1))
+        stage = ctx.enter_context(tc.tile_pool(name="stage", bufs=2))
+        gates = ctx.enter_context(tc.tile_pool(name="gates", bufs=3 * CHUNKS))
+        work = ctx.enter_context(tc.tile_pool(name="work", bufs=2))
+        z_banks = ctx.enter_context(tc.psum_pool(name="z_banks", bufs=4))
+        t_banks = ctx.enter_context(tc.psum_pool(name="t_banks", bufs=4))
+
+        ident = consts.tile([P, P], FP32)
+        w_words = consts.tile([P, 2, 2 * 3 * WIDTH], U8, align_bytes=64)
+        w_scales = consts.tile([P, 2, 3 * WIDTH], U8, align_bytes=64)
+        bias_rows = consts.tile([P, P], BF16)
+        bias_rows_f32 = consts.tile([P, P], FP32)
+        bias_T = consts.tile([P, 3 * CHUNKS], FP32)
+        warm = consts.tile([P, 1], FP32)
+        x_sb = consts.tile([P, WIDTH], BF16)
+        x_codes = consts.tile([P, PASS_COLS], U32, align_bytes=64)
+        x_scales = consts.tile([P, PASS_COLS], U8, align_bytes=64)
+        h_codes = consts.tile([P, N_GROUPS, PASS_COLS], U32, align_bytes=64)
+        h_scales = consts.tile([P, N_GROUPS, PASS_COLS], U8, align_bytes=64)
+        h_sb = [loads.tile([P, GROUP_COLS], BF16, name="h_sb%d" % g) for g in range(N_GROUPS)]
+        c_sb = [loads.tile([P, GROUP_COLS], BF16, name="c_sb%d" % g) for g in range(N_GROUPS)]
+        u_sb = [loads.tile([P, GROUP_COLS], BF16, name="u_sb%d" % g) for g in range(N_GROUPS)]
+
+        nc.vector.memset(bias_rows[:], 0.0)
+        nc.vector.memset(w_scales[:].bitcast(I32), 0)
+        nc.vector.memset(warm[:], 0.0)
+        make_identity(nc, ident[:])
+        nc.scalar.activation(out=warm[:], in_=warm[:], func=SIGMOID)
+
+        def group_cols(g):
+            return slice(g * GROUP_COLS, (g + 1) * GROUP_COLS)
+
+        nc.sync.dma_start(out=x_sb[:], in_=inputs)
+        nc.sync.dma_start(out=h_sb[0][:], in_=h_state[:, group_cols(0)])
+        nc.sync.dma_start(out=u_sb[0][:], in_=c_upd_rows[:, group_cols(0)])
+        nc.sync.dma_start(out=bias_rows[0 : 3 * CHUNKS, :], in_=bias.rearrange("(j p) -> j p", p=P))
+        for w, scales in ((W_H, recurrent_kernel_scales), (W_X, kernel_scales)):
+            for quad in range(4):
+                nc.sync.dma_start(
+                    out=w_scales[32 * quad : 32 * quad + 4, w, :].bitcast(I32),
+                    in_=scales[0, 4 * quad : 4 * quad + 4, :].bitcast(I32),
+                )
+        nc.sync.dma_start(out=w_words[:, W_H, :].bitcast(I32), in_=recurrent_kernel_words[0].bitcast(I32))
+        nc.sync.dma_start(out=w_words[:, W_X, :].bitcast(I32), in_=kernel_words[0].bitcast(I32))
+        for g in range(N_GROUPS):
+            if g + 1 < N_GROUPS:
+                nc.sync.dma_start(out=h_sb[g + 1][:], in_=h_state[:, group_cols(g + 1)])
+                nc.sync.dma_start(out=u_sb[g + 1][:], in_=c_upd_rows[:, group_cols(g + 1)])
+            nc.sync.dma_start(out=c_sb[g][:], in_=c_state[:, group_cols(g)])
+
+        def turn_slots(rows, slot_list, grouped_words, repeat):
+            turned = t_banks.tile([P, len(slot_list), 2, P], FP32, tag="t_bank")
+            for n, s in enumerate(slot_list):
+                for u in range(2):
+                    nc.tensor.transpose(
+                        turned[:, n, u, :], rows[:, s * WORDS + u : (s + 1) * WORDS : 2], ident[:]
+                    )
+            by_row = turned[:].rearrange("p s u b -> p s b u")
+            if repeat > 1:
+                by_row = by_row.to_broadcast([P, repeat, P, 2])
+            nc.vector.tensor_copy(out=grouped_words, in_=by_row)
+
+        def new_grouped():
+            grouped = stage.tile([P, 4 * PASS_COLS], BF16, name="grouped", align_bytes=64)
+            words = grouped[:].bitcast(FP32).rearrange("p (s b u) -> p s b u", s=GROUP_SLOTS, b=P, u=2)
+            return grouped, words
+
+        grouped_of = {}
+
+        def turn_h(g):
+            grouped, words = new_grouped()
+            rows = h_sb[g][:].bitcast(FP32)
+            turn_slots(rows, [0, 1], words[:, 0:2], 1)
+            turn_slots(rows, [2, 3], words[:, 2:4], 1)
+            grouped_of[g] = grouped
+
+        def quantise_h(g):
+            nc.vector.quantize_mx(
+                out=h_codes[:, g, :].bitcast(E4M3X4), scales=h_scales[:, g, :], in_=grouped_of[g][:]
+            )
+
+        x_grouped, x_grouped_words = new_grouped()
+        turn_slots(x_sb[:].bitcast(FP32), [0], x_grouped_words, GROUP_SLOTS)
+        turn_h(0)
+        nc.vector.quantize_mx(out=x_codes[:].bitcast(E4M3X4), scales=x_scales[:], in_=x_grouped[:])
+        nc.vector.tensor_copy(out=bias_rows_f32[:], in_=bias_rows[:])
+        bias_bank = t_banks.tile([P, P], FP32, tag="t_bank")
+        nc.tensor.transpose(bias_bank[:], bias_rows_f32[:], ident[:])
+        quantise_h(0)
+        nc.vector.tensor_copy(out=bias_T[:], in_=bias_bank[:, 0 : 3 * CHUNKS])
+
+        cand = {}
+        i_cand = {}
+        c_new = {}
+        tanh_c = {}
+
+        def tanh_candidate(g):
+            cand[g] = work.tile([P, GROUP_COLS], FP32, name="cand")
+            nc.scalar.activation(out=cand[g][:], in_=u_sb[g][:], func=TANH)
+
+        def tanh_cell(g):
+            tanh_c[g] = work.tile([P, GROUP_COLS], FP32, name="tanh_c")
+            nc.scalar.activation(out=tanh_c[g][:], in_=c_new[g][:], func=TANH)
+
+        def squash(gate, g):
+            gate_T = []
+            for j in range(CHUNKS):
+                chunk = gate * CHUNKS + j
+                z_T = z_banks.tile([P, PASS_COLS], FP32, name="z_T")
+                for w, codes, scales in (
+                    (W_X, x_codes[:], x_scales[:]),
+                    (W_H, h_codes[:, g, :], h_scales[:, g, :]),
+                ):
+                    nc.tensor.matmul_mx(
+                        out=z_T[:],
+                        lhsT=w_words[:, w, 2 * P * chunk : 2 * P * (chunk + 1)].bitcast(E2M1X4),
+                        lhsT_scale=w_scales[:, w, P * chunk : P * (chunk + 1)],
+                        rhs=codes.bitcast(E4M3X4),
+                        rhs_scale=scales,
+                        start=(w == W_X),
+                        stop=(w == W_H),
+                    )
+                squashed = gates.tile([P, PASS_COLS], FP32, name="squashed")
+                nc.scalar.activation(
+                    out=squashed[:], in_=z_T[:], func=SIGMOID, bias=bias_T[:, chunk : chunk + 1], scale=1.0
+                )
+                gate_T.append(squashed)
+            return gate_T
+
+        def use(gate, g, gate_T):
+            if gate == GATE_I:
+                i_cand[g] = work.tile([P, GROUP_COLS], FP32, name="i_cand")
+                product, partner = i_cand[g], cand[g]
+            elif gate == GATE_F:
+                c_new[g] = work.tile([P, GROUP_COLS], FP32, name="c_new")
+                product, partner = c_new[g], c_sb[g]
+            else:
+                product = work.tile([P, GROUP_COLS], FP32, name="h_new")
+                partner = tanh_c[g]
+            for s in range(GROUP_SLOTS):
+                cols = slice(s * WIDTH, (s + 1) * WIDTH)
+                bank = t_banks.tile([P, WIDTH], FP32, tag="t_bank")
+                for j in range(CHUNKS):
+                    nc.tensor.transpose(
+                        bank[:, j * P : (j + 1) * P], gate_T[j][:, s * P : (s + 1) * P], ident[:]
+                    )
+                nc.vector.tensor_tensor(out=product[:, cols], in0=bank[:], in1=partner[:, cols], op=MULT)
+                if gate == GATE_O:
+                    first = g * GROUP_COLS + s * WIDTH
+                    nc.sync.dma_start(out=out_0[:, first : first + WIDTH], in_=product[:, cols])
+            if gate == GATE_F:
+                nc.vector.tensor_tensor(out=c_new[g][:], in0=c_new[g][:], in1=i_cand[g][:], op=ADD)
+                nc.sync.dma_start(out=out_1[:, group_cols(g)], in_=c_new[g][:])
+
+        steps = []
+        for r in range(N_GROUPS + O_LAG):
+            if r < N_GROUPS:
+                steps.append((GATE_I, r))
+                steps.append((GATE_F, r))
+            if r >= O_LAG:
+                steps.append((GATE_O, r - O_LAG))
+
+        tanh_candidate(0)
+        squashed_before = None
+        for n, (gate, g) in enumerate(steps):
+            gate_T = squash(gate, g)
+            if gate == GATE_F and g + 1 < N_GROUPS:
+                tanh_candidate(g + 1)
+                quantise_h(g + 1)
+            if n >= 2 and steps[n - 2][0] == GATE_F:
+                tanh_cell(steps[n - 2][1])
+            if gate == GATE_I and g + 1 < N_GROUPS:
+                turn_h(g + 1)
+            if squashed_before is not None:
+                use(*squashed_before)
+            squashed_before = (gate, g, gate_T)
+        use(*squashed_before)

@@ -23,10 +23,12 @@ CHUNKS = WIDTH // P
 GROUP_SLOTS = 4
 N_GROUPS = SLOTS // GROUP_SLOTS
 GROUP_COLS = GROUP_SLOTS * WIDTH
+HALF_COLS = GROUP_COLS // 2
 PASS_COLS = GROUP_SLOTS * P
 WORDS = WIDTH // 2
 W_X, W_H = 0, 1
 O_LAG = 1
+EARLY_CANDS = 3
 
 FLOPS = 2 * WIDTH * 3 * WIDTH * (P + P * SLOTS)
 
@@ -53,8 +55,9 @@ def tile_rlstmcell_pb_kernel(
         consts = ctx.enter_context(tc.tile_pool(name="consts", bufs=1))
         loads = ctx.enter_context(tc.tile_pool(name="loads", bufs=1))
         stage = ctx.enter_context(tc.tile_pool(name="stage", bufs=2))
-        gates = ctx.enter_context(tc.tile_pool(name="gates", bufs=3 * CHUNKS))
+        gates = ctx.enter_context(tc.tile_pool(name="gates", bufs=2 * CHUNKS))
         work = ctx.enter_context(tc.tile_pool(name="work", bufs=2))
+        cands = ctx.enter_context(tc.tile_pool(name="cands", bufs=N_GROUPS))
         z_banks = ctx.enter_context(tc.psum_pool(name="z_banks", bufs=4))
         t_banks = ctx.enter_context(tc.psum_pool(name="t_banks", bufs=4))
 
@@ -64,6 +67,8 @@ def tile_rlstmcell_pb_kernel(
         bias_rows = consts.tile([P, P], BF16)
         bias_rows_f32 = consts.tile([P, P], FP32)
         bias_T = consts.tile([P, 3 * CHUNKS], FP32)
+        bias_i = consts.tile([P, WIDTH], BF16)
+        x_part_i = consts.tile([P, WIDTH], FP32)
         warm = consts.tile([P, 1], FP32)
         x_sb = consts.tile([P, WIDTH], BF16)
         x_codes = consts.tile([P, PASS_COLS], U32, align_bytes=64)
@@ -86,6 +91,7 @@ def tile_rlstmcell_pb_kernel(
         nc.sync.dma_start(out=x_sb[:], in_=inputs)
         nc.sync.dma_start(out=h_sb[0][:], in_=h_state[:, group_cols(0)])
         nc.sync.dma_start(out=u_sb[0][:], in_=c_upd_rows[:, group_cols(0)])
+        nc.sync.dma_start(out=u_sb[1][:], in_=c_upd_rows[:, group_cols(1)])
         nc.sync.dma_start(out=bias_rows[0 : 3 * CHUNKS, :], in_=bias.rearrange("(j p) -> j p", p=P))
         for w, scales in ((W_H, recurrent_kernel_scales), (W_X, kernel_scales)):
             for quad in range(4):
@@ -95,11 +101,15 @@ def tile_rlstmcell_pb_kernel(
                 )
         nc.sync.dma_start(out=w_words[:, W_H, :].bitcast(I32), in_=recurrent_kernel_words[0].bitcast(I32))
         nc.sync.dma_start(out=w_words[:, W_X, :].bitcast(I32), in_=kernel_words[0].bitcast(I32))
-        for g in range(N_GROUPS):
-            if g + 1 < N_GROUPS:
-                nc.sync.dma_start(out=h_sb[g + 1][:], in_=h_state[:, group_cols(g + 1)])
-                nc.sync.dma_start(out=u_sb[g + 1][:], in_=c_upd_rows[:, group_cols(g + 1)])
-            nc.sync.dma_start(out=c_sb[g][:], in_=c_state[:, group_cols(g)])
+        nc.sync.dma_start(out=bias_i[:], in_=bias[0:WIDTH].partition_broadcast(P))
+        nc.sync.dma_start(out=u_sb[2][:], in_=c_upd_rows[:, group_cols(2)])
+        nc.sync.dma_start(out=h_sb[1][:], in_=h_state[:, group_cols(1)])
+        nc.sync.dma_start(out=c_sb[0][:], in_=c_state[:, group_cols(0)])
+        nc.sync.dma_start(out=u_sb[3][:], in_=c_upd_rows[:, group_cols(3)])
+        for g in range(2, N_GROUPS):
+            nc.sync.dma_start(out=h_sb[g][:], in_=h_state[:, group_cols(g)])
+            nc.sync.dma_start(out=c_sb[g - 1][:], in_=c_state[:, group_cols(g - 1)])
+        nc.sync.dma_start(out=c_sb[N_GROUPS - 1][:], in_=c_state[:, group_cols(N_GROUPS - 1)])
 
         def turn_slots(rows, slot_list, grouped_words, repeat):
             turned = t_banks.tile([P, len(slot_list), 2, P], FP32, tag="t_bank")
@@ -148,12 +158,39 @@ def tile_rlstmcell_pb_kernel(
         tanh_c = {}
 
         def tanh_candidate(g):
-            cand[g] = work.tile([P, GROUP_COLS], FP32, name="cand")
+            cand[g] = cands.tile([P, GROUP_COLS], FP32, name="cand")
             nc.scalar.activation(out=cand[g][:], in_=u_sb[g][:], func=TANH)
 
         def tanh_cell(g):
             tanh_c[g] = work.tile([P, GROUP_COLS], FP32, name="tanh_c")
-            nc.scalar.activation(out=tanh_c[g][:], in_=c_new[g][:], func=TANH)
+            for s in range(GROUP_SLOTS):
+                cols = slice(s * WIDTH, (s + 1) * WIDTH)
+                nc.scalar.activation(out=tanh_c[g][:, cols], in_=c_new[g][:, cols], func=TANH)
+
+        def input_gate(g):
+            gate_i = work.tile([P, GROUP_COLS], FP32, name="gate_i")
+            for s in range(GROUP_SLOTS):
+                bank = t_banks.tile([P, WIDTH], FP32, tag="t_bank")
+                nc.tensor.matmul_mx(
+                    out=bank[:],
+                    lhsT=h_codes[:, g, s * P : (s + 1) * P].bitcast(E4M3X4),
+                    lhsT_scale=h_scales[:, g, s * P : (s + 1) * P],
+                    rhs=w_words[:, W_H, 0 : 2 * WIDTH].bitcast(E2M1X4),
+                    rhs_scale=w_scales[:, W_H, 0:WIDTH],
+                    start=True,
+                    stop=True,
+                )
+                nc.vector.tensor_tensor(
+                    out=gate_i[:, s * WIDTH : (s + 1) * WIDTH], in0=bank[:], in1=x_part_i[:], op=ADD
+                )
+            return gate_i
+
+        def finish_input_gate(g, gate_i):
+            nc.scalar.activation(out=gate_i[:], in_=gate_i[:], func=SIGMOID)
+            i_cand[g] = work.tile([P, GROUP_COLS], FP32, name="i_cand")
+            for s in range(GROUP_SLOTS):
+                cols = slice(s * WIDTH, (s + 1) * WIDTH)
+                nc.gpsimd.tensor_tensor(out=i_cand[g][:, cols], in0=gate_i[:, cols], in1=cand[g][:, cols], op=MULT)
 
         def squash(gate, g):
             gate_T = []
@@ -181,10 +218,7 @@ def tile_rlstmcell_pb_kernel(
             return gate_T
 
         def use(gate, g, gate_T):
-            if gate == GATE_I:
-                i_cand[g] = work.tile([P, GROUP_COLS], FP32, name="i_cand")
-                product, partner = i_cand[g], cand[g]
-            elif gate == GATE_F:
+            if gate == GATE_F:
                 c_new[g] = work.tile([P, GROUP_COLS], FP32, name="c_new")
                 product, partner = c_new[g], c_sb[g]
             else:
@@ -202,29 +236,48 @@ def tile_rlstmcell_pb_kernel(
                     first = g * GROUP_COLS + s * WIDTH
                     nc.sync.dma_start(out=out_0[:, first : first + WIDTH], in_=product[:, cols])
             if gate == GATE_F:
-                nc.vector.tensor_tensor(out=c_new[g][:], in0=c_new[g][:], in1=i_cand[g][:], op=ADD)
-                nc.sync.dma_start(out=out_1[:, group_cols(g)], in_=c_new[g][:])
+                for half, engine in enumerate((nc.vector, nc.gpsimd)):
+                    cols = slice(half * HALF_COLS, (half + 1) * HALF_COLS)
+                    engine.tensor_tensor(out=c_new[g][:, cols], in0=c_new[g][:, cols], in1=i_cand[g][:, cols], op=ADD)
+                    first = g * GROUP_COLS + half * HALF_COLS
+                    nc.sync.dma_start(out=out_1[:, first : first + HALF_COLS], in_=c_new[g][:, cols])
 
-        steps = []
+        x_bank = t_banks.tile([P, WIDTH], FP32, tag="t_bank")
+        nc.tensor.matmul_mx(
+            out=x_bank[:],
+            lhsT=x_codes[:, 0:P].bitcast(E4M3X4),
+            lhsT_scale=x_scales[:, 0:P],
+            rhs=w_words[:, W_X, 0 : 2 * WIDTH].bitcast(E2M1X4),
+            rhs_scale=w_scales[:, W_X, 0:WIDTH],
+            start=True,
+            stop=True,
+        )
+        nc.vector.tensor_tensor(out=x_part_i[:], in0=x_bank[:], in1=bias_i[:], op=ADD)
+
+        for g in range(EARLY_CANDS):
+            tanh_candidate(g)
+        finish_input_gate(0, input_gate(0))
+        turn_h(1)
+        quantise_h(1)
+
+        o_T = None
         for r in range(N_GROUPS + O_LAG):
             if r < N_GROUPS:
-                steps.append((GATE_I, r))
-                steps.append((GATE_F, r))
+                f_T = squash(GATE_F, r)
+            if r + 1 < N_GROUPS:
+                gate_i = input_gate(r + 1)
+                finish_input_gate(r + 1, gate_i)
+            if r + EARLY_CANDS < N_GROUPS:
+                tanh_candidate(r + EARLY_CANDS)
+            if r + 2 < N_GROUPS:
+                turn_h(r + 2)
+            if o_T is not None:
+                use(GATE_O, r - O_LAG - 1, o_T)
+            if r + 2 < N_GROUPS:
+                quantise_h(r + 2)
             if r >= O_LAG:
-                steps.append((GATE_O, r - O_LAG))
-
-        tanh_candidate(0)
-        squashed_before = None
-        for n, (gate, g) in enumerate(steps):
-            gate_T = squash(gate, g)
-            if gate == GATE_F and g + 1 < N_GROUPS:
-                tanh_candidate(g + 1)
-                quantise_h(g + 1)
-            if n >= 2 and steps[n - 2][0] == GATE_F:
-                tanh_cell(steps[n - 2][1])
-            if gate == GATE_I and g + 1 < N_GROUPS:
-                turn_h(g + 1)
-            if squashed_before is not None:
-                use(*squashed_before)
-            squashed_before = (gate, g, gate_T)
-        use(*squashed_before)
+                o_T = squash(GATE_O, r - O_LAG)
+                tanh_cell(r - O_LAG)
+            if r < N_GROUPS:
+                use(GATE_F, r, f_T)
+        use(GATE_O, N_GROUPS - 1, o_T)

@@ -67,8 +67,10 @@ def tile_rlstmcell_pb_kernel(
         bias_rows = consts.tile([P, P], BF16)
         bias_rows_f32 = consts.tile([P, P], FP32)
         bias_T = consts.tile([P, 3 * CHUNKS], FP32)
-        bias_i = consts.tile([P, WIDTH], BF16)
+        bias_i = consts.tile([P, WIDTH], FP32)
         x_part_i = consts.tile([P, WIDTH], FP32)
+        bias_row0 = consts.tile([P, WIDTH], BF16)
+        ones = consts.tile([P, P], BF16)
         warm = consts.tile([P, 1], FP32)
         x_sb = consts.tile([P, WIDTH], BF16)
         x_codes = consts.tile([P, PASS_COLS], U32, align_bytes=64)
@@ -80,6 +82,8 @@ def tile_rlstmcell_pb_kernel(
         u_sb = [loads.tile([P, GROUP_COLS], BF16, name="u_sb%d" % g) for g in range(N_GROUPS)]
 
         nc.vector.memset(bias_rows[:], 0.0)
+        nc.vector.memset(bias_row0[:], 0.0)
+        nc.vector.memset(ones[:], 1.0)
         nc.vector.memset(w_scales[:].bitcast(I32), 0)
         nc.vector.memset(warm[:], 0.0)
         make_identity(nc, ident[:])
@@ -88,28 +92,32 @@ def tile_rlstmcell_pb_kernel(
         def group_cols(g):
             return slice(g * GROUP_COLS, (g + 1) * GROUP_COLS)
 
-        nc.sync.dma_start(out=x_sb[:], in_=inputs)
-        nc.sync.dma_start(out=h_sb[0][:], in_=h_state[:, group_cols(0)])
-        nc.sync.dma_start(out=u_sb[0][:], in_=c_upd_rows[:, group_cols(0)])
-        nc.sync.dma_start(out=u_sb[1][:], in_=c_upd_rows[:, group_cols(1)])
-        nc.sync.dma_start(out=bias_rows[0 : 3 * CHUNKS, :], in_=bias.rearrange("(j p) -> j p", p=P))
-        for w, scales in ((W_H, recurrent_kernel_scales), (W_X, kernel_scales)):
+        def load_scales(w, scales):
             for quad in range(4):
                 nc.sync.dma_start(
                     out=w_scales[32 * quad : 32 * quad + 4, w, :].bitcast(I32),
                     in_=scales[0, 4 * quad : 4 * quad + 4, :].bitcast(I32),
                 )
+
+        nc.sync.dma_start(out=x_sb[:], in_=inputs)
+        nc.sync.dma_start(out=h_sb[0][:], in_=h_state[:, group_cols(0)])
+        nc.sync.dma_start(out=u_sb[0][:], in_=c_upd_rows[:, group_cols(0)])
+        nc.sync.dma_start(out=bias_rows[0 : 3 * CHUNKS, :], in_=bias.rearrange("(j p) -> j p", p=P))
+        nc.sync.dma_start(out=bias_row0[0:1, :], in_=bias[0:WIDTH].unsqueeze(0))
         nc.sync.dma_start(out=w_words[:, W_H, :].bitcast(I32), in_=recurrent_kernel_words[0].bitcast(I32))
         nc.sync.dma_start(out=w_words[:, W_X, :].bitcast(I32), in_=kernel_words[0].bitcast(I32))
-        nc.sync.dma_start(out=bias_i[:], in_=bias[0:WIDTH].partition_broadcast(P))
-        nc.sync.dma_start(out=u_sb[2][:], in_=c_upd_rows[:, group_cols(2)])
+        load_scales(W_H, recurrent_kernel_scales)
+        load_scales(W_X, kernel_scales)
+        nc.sync.dma_start(out=u_sb[1][:], in_=c_upd_rows[:, group_cols(1)])
         nc.sync.dma_start(out=h_sb[1][:], in_=h_state[:, group_cols(1)])
+        nc.sync.dma_start(out=u_sb[2][:], in_=c_upd_rows[:, group_cols(2)])
         nc.sync.dma_start(out=c_sb[0][:], in_=c_state[:, group_cols(0)])
         nc.sync.dma_start(out=u_sb[3][:], in_=c_upd_rows[:, group_cols(3)])
-        for g in range(2, N_GROUPS):
-            nc.sync.dma_start(out=h_sb[g][:], in_=h_state[:, group_cols(g)])
-            nc.sync.dma_start(out=c_sb[g - 1][:], in_=c_state[:, group_cols(g - 1)])
-        nc.sync.dma_start(out=c_sb[N_GROUPS - 1][:], in_=c_state[:, group_cols(N_GROUPS - 1)])
+        nc.sync.dma_start(out=h_sb[2][:], in_=h_state[:, group_cols(2)])
+        nc.sync.dma_start(out=c_sb[1][:], in_=c_state[:, group_cols(1)])
+        nc.sync.dma_start(out=h_sb[3][:], in_=h_state[:, group_cols(3)])
+        nc.sync.dma_start(out=c_sb[2][:], in_=c_state[:, group_cols(2)])
+        nc.sync.dma_start(out=c_sb[3][:], in_=c_state[:, group_cols(3)])
 
         def turn_slots(rows, slot_list, grouped_words, repeat):
             turned = t_banks.tile([P, len(slot_list), 2, P], FP32, tag="t_bank")
@@ -151,6 +159,9 @@ def tile_rlstmcell_pb_kernel(
         nc.tensor.transpose(bias_bank[:], bias_rows_f32[:], ident[:])
         quantise_h(0)
         nc.vector.tensor_copy(out=bias_T[:], in_=bias_bank[:, 0 : 3 * CHUNKS])
+        spread_bank = t_banks.tile([P, WIDTH], FP32, tag="t_bank")
+        nc.tensor.matmul(out=spread_bank[:], lhsT=ones[:], rhs=bias_row0[:], start=True, stop=True)
+        nc.vector.tensor_copy(out=bias_i[:], in_=spread_bank[:])
 
         cand = {}
         i_cand = {}
@@ -254,30 +265,34 @@ def tile_rlstmcell_pb_kernel(
         )
         nc.vector.tensor_tensor(out=x_part_i[:], in0=x_bank[:], in1=bias_i[:], op=ADD)
 
-        for g in range(EARLY_CANDS):
+        gate_i_of = {}
+        for g in range(2):
             tanh_candidate(g)
-        finish_input_gate(0, input_gate(0))
+        gate_i_of[0] = input_gate(0)
+        finish_input_gate(0, gate_i_of[0])
         turn_h(1)
         quantise_h(1)
 
-        o_T = None
-        for r in range(N_GROUPS + O_LAG):
+        o_T_of = {}
+        for r in range(N_GROUPS + 1):
             if r < N_GROUPS:
                 f_T = squash(GATE_F, r)
-            if r + 1 < N_GROUPS:
-                gate_i = input_gate(r + 1)
-                finish_input_gate(r + 1, gate_i)
-            if r + EARLY_CANDS < N_GROUPS:
-                tanh_candidate(r + EARLY_CANDS)
+            if r >= 2:
+                use(GATE_O, r - 2, o_T_of[r - 2])
+            if r >= 1:
+                o_T_of[r - 1] = squash(GATE_O, r - 1)
+            if r + 2 < N_GROUPS:
+                tanh_candidate(r + 2)
+            if r >= 1:
+                tanh_cell(r - 1)
             if r + 2 < N_GROUPS:
                 turn_h(r + 2)
-            if o_T is not None:
-                use(GATE_O, r - O_LAG - 1, o_T)
+            if r + 1 < N_GROUPS:
+                gate_i_of[r + 1] = input_gate(r + 1)
             if r + 2 < N_GROUPS:
                 quantise_h(r + 2)
-            if r >= O_LAG:
-                o_T = squash(GATE_O, r - O_LAG)
-                tanh_cell(r - O_LAG)
             if r < N_GROUPS:
                 use(GATE_F, r, f_T)
-        use(GATE_O, N_GROUPS - 1, o_T)
+            if r + 1 < N_GROUPS:
+                finish_input_gate(r + 1, gate_i_of[r + 1])
+        use(GATE_O, N_GROUPS - 1, o_T_of[N_GROUPS - 1])

@@ -18,6 +18,7 @@ ADD = mybir.AluOpType.add
 P = 128
 SLOTS = 16
 WIDTH = 512
+GATES = 3
 GATE_I, GATE_F, GATE_O = 0, 1, 2
 CHUNKS = WIDTH // P
 GROUP_SLOTS = 4
@@ -27,10 +28,11 @@ HALF_COLS = GROUP_COLS // 2
 PASS_COLS = GROUP_SLOTS * P
 WORDS = WIDTH // 2
 W_X, W_H = 0, 1
-O_LAG = 1
-EARLY_CANDS = 3
+QUADS = 4
+PSUM_BANKS = 8
+EARLY_CANDS = 2
 
-FLOPS = 2 * WIDTH * 3 * WIDTH * (P + P * SLOTS)
+FLOPS = 2 * WIDTH * GATES * WIDTH * (P + P * SLOTS)
 
 
 def tile_rlstmcell_pb_kernel(
@@ -58,15 +60,15 @@ def tile_rlstmcell_pb_kernel(
         gates = ctx.enter_context(tc.tile_pool(name="gates", bufs=2 * CHUNKS))
         work = ctx.enter_context(tc.tile_pool(name="work", bufs=2))
         cands = ctx.enter_context(tc.tile_pool(name="cands", bufs=N_GROUPS))
-        z_banks = ctx.enter_context(tc.psum_pool(name="z_banks", bufs=4))
-        t_banks = ctx.enter_context(tc.psum_pool(name="t_banks", bufs=4))
+        z_banks = ctx.enter_context(tc.psum_pool(name="z_banks", bufs=PSUM_BANKS // 2))
+        t_banks = ctx.enter_context(tc.psum_pool(name="t_banks", bufs=PSUM_BANKS // 2))
 
         ident = consts.tile([P, P], FP32)
-        w_words = consts.tile([P, 2, 2 * 3 * WIDTH], U8, align_bytes=64)
-        w_scales = consts.tile([P, 2, 3 * WIDTH], U8, align_bytes=64)
+        w_words = consts.tile([P, 2, 2 * GATES * WIDTH], U8, align_bytes=64)
+        w_scales = consts.tile([P, 2, GATES * WIDTH], U8, align_bytes=64)
         bias_rows = consts.tile([P, P], BF16)
         bias_rows_f32 = consts.tile([P, P], FP32)
-        bias_T = consts.tile([P, 3 * CHUNKS], FP32)
+        bias_T = consts.tile([P, GATES * CHUNKS], FP32)
         bias_i = consts.tile([P, WIDTH], FP32)
         x_part_i = consts.tile([P, WIDTH], FP32)
         bias_row0 = consts.tile([P, WIDTH], BF16)
@@ -92,32 +94,41 @@ def tile_rlstmcell_pb_kernel(
         def group_cols(g):
             return slice(g * GROUP_COLS, (g + 1) * GROUP_COLS)
 
+        def load_h(g):
+            nc.sync.dma_start(out=h_sb[g][:], in_=h_state[:, group_cols(g)])
+
+        def load_c_upd(g):
+            nc.sync.dma_start(out=u_sb[g][:], in_=c_upd_rows[:, group_cols(g)])
+
+        def load_c(g):
+            nc.sync.dma_start(out=c_sb[g][:], in_=c_state[:, group_cols(g)])
+
         def load_scales(w, scales):
-            for quad in range(4):
+            for quad in range(QUADS):
                 nc.sync.dma_start(
                     out=w_scales[32 * quad : 32 * quad + 4, w, :].bitcast(I32),
                     in_=scales[0, 4 * quad : 4 * quad + 4, :].bitcast(I32),
                 )
 
         nc.sync.dma_start(out=x_sb[:], in_=inputs)
-        nc.sync.dma_start(out=h_sb[0][:], in_=h_state[:, group_cols(0)])
-        nc.sync.dma_start(out=u_sb[0][:], in_=c_upd_rows[:, group_cols(0)])
-        nc.sync.dma_start(out=bias_rows[0 : 3 * CHUNKS, :], in_=bias.rearrange("(j p) -> j p", p=P))
-        nc.sync.dma_start(out=bias_row0[0:1, :], in_=bias[0:WIDTH].unsqueeze(0))
+        load_h(0)
+        load_c_upd(0)
+        nc.sync.dma_start(out=bias_rows[0 : GATES * CHUNKS, :], in_=bias.rearrange("(j p) -> j p", p=P))
+        nc.sync.dma_start(out=bias_row0[0:1, :], in_=bias[GATE_I * WIDTH : (GATE_I + 1) * WIDTH].unsqueeze(0))
         nc.sync.dma_start(out=w_words[:, W_H, :].bitcast(I32), in_=recurrent_kernel_words[0].bitcast(I32))
         nc.sync.dma_start(out=w_words[:, W_X, :].bitcast(I32), in_=kernel_words[0].bitcast(I32))
         load_scales(W_H, recurrent_kernel_scales)
         load_scales(W_X, kernel_scales)
-        nc.sync.dma_start(out=u_sb[1][:], in_=c_upd_rows[:, group_cols(1)])
-        nc.sync.dma_start(out=h_sb[1][:], in_=h_state[:, group_cols(1)])
-        nc.sync.dma_start(out=u_sb[2][:], in_=c_upd_rows[:, group_cols(2)])
-        nc.sync.dma_start(out=c_sb[0][:], in_=c_state[:, group_cols(0)])
-        nc.sync.dma_start(out=u_sb[3][:], in_=c_upd_rows[:, group_cols(3)])
-        nc.sync.dma_start(out=h_sb[2][:], in_=h_state[:, group_cols(2)])
-        nc.sync.dma_start(out=c_sb[1][:], in_=c_state[:, group_cols(1)])
-        nc.sync.dma_start(out=h_sb[3][:], in_=h_state[:, group_cols(3)])
-        nc.sync.dma_start(out=c_sb[2][:], in_=c_state[:, group_cols(2)])
-        nc.sync.dma_start(out=c_sb[3][:], in_=c_state[:, group_cols(3)])
+        load_c_upd(1)
+        load_h(1)
+        load_c_upd(2)
+        load_c(0)
+        load_c_upd(3)
+        load_h(2)
+        load_c(1)
+        load_h(3)
+        load_c(2)
+        load_c(3)
 
         def turn_slots(rows, slot_list, grouped_words, repeat):
             turned = t_banks.tile([P, len(slot_list), 2, P], FP32, tag="t_bank")
@@ -158,7 +169,7 @@ def tile_rlstmcell_pb_kernel(
         bias_bank = t_banks.tile([P, P], FP32, tag="t_bank")
         nc.tensor.transpose(bias_bank[:], bias_rows_f32[:], ident[:])
         quantise_h(0)
-        nc.vector.tensor_copy(out=bias_T[:], in_=bias_bank[:, 0 : 3 * CHUNKS])
+        nc.vector.tensor_copy(out=bias_T[:], in_=bias_bank[:, 0 : GATES * CHUNKS])
         spread_bank = t_banks.tile([P, WIDTH], FP32, tag="t_bank")
         nc.tensor.matmul(out=spread_bank[:], lhsT=ones[:], rhs=bias_row0[:], start=True, stop=True)
         nc.vector.tensor_copy(out=bias_i[:], in_=spread_bank[:])
@@ -178,6 +189,12 @@ def tile_rlstmcell_pb_kernel(
                 cols = slice(s * WIDTH, (s + 1) * WIDTH)
                 nc.scalar.activation(out=tanh_c[g][:, cols], in_=c_new[g][:, cols], func=TANH)
 
+        def gate_words(w, gate):
+            return w_words[:, w, 2 * WIDTH * gate : 2 * WIDTH * (gate + 1)].bitcast(E2M1X4)
+
+        def gate_scales(w, gate):
+            return w_scales[:, w, WIDTH * gate : WIDTH * (gate + 1)]
+
         def input_gate(g):
             gate_i = work.tile([P, GROUP_COLS], FP32, name="gate_i")
             for s in range(GROUP_SLOTS):
@@ -186,8 +203,8 @@ def tile_rlstmcell_pb_kernel(
                     out=bank[:],
                     lhsT=h_codes[:, g, s * P : (s + 1) * P].bitcast(E4M3X4),
                     lhsT_scale=h_scales[:, g, s * P : (s + 1) * P],
-                    rhs=w_words[:, W_H, 0 : 2 * WIDTH].bitcast(E2M1X4),
-                    rhs_scale=w_scales[:, W_H, 0:WIDTH],
+                    rhs=gate_words(W_H, GATE_I),
+                    rhs_scale=gate_scales(W_H, GATE_I),
                     start=True,
                     stop=True,
                 )
@@ -258,15 +275,15 @@ def tile_rlstmcell_pb_kernel(
             out=x_bank[:],
             lhsT=x_codes[:, 0:P].bitcast(E4M3X4),
             lhsT_scale=x_scales[:, 0:P],
-            rhs=w_words[:, W_X, 0 : 2 * WIDTH].bitcast(E2M1X4),
-            rhs_scale=w_scales[:, W_X, 0:WIDTH],
+            rhs=gate_words(W_X, GATE_I),
+            rhs_scale=gate_scales(W_X, GATE_I),
             start=True,
             stop=True,
         )
         nc.vector.tensor_tensor(out=x_part_i[:], in0=x_bank[:], in1=bias_i[:], op=ADD)
 
         gate_i_of = {}
-        for g in range(2):
+        for g in range(EARLY_CANDS):
             tanh_candidate(g)
         gate_i_of[0] = input_gate(0)
         finish_input_gate(0, gate_i_of[0])
@@ -274,15 +291,14 @@ def tile_rlstmcell_pb_kernel(
         quantise_h(1)
 
         o_T_of = {}
-        for r in range(N_GROUPS + 1):
-            if r < N_GROUPS:
-                f_T = squash(GATE_F, r)
+        for r in range(N_GROUPS):
+            f_T = squash(GATE_F, r)
             if r >= 2:
                 use(GATE_O, r - 2, o_T_of[r - 2])
             if r >= 1:
                 o_T_of[r - 1] = squash(GATE_O, r - 1)
-            if r + 2 < N_GROUPS:
-                tanh_candidate(r + 2)
+            if r + EARLY_CANDS < N_GROUPS:
+                tanh_candidate(r + EARLY_CANDS)
             if r >= 1:
                 tanh_cell(r - 1)
             if r + 2 < N_GROUPS:
@@ -291,8 +307,12 @@ def tile_rlstmcell_pb_kernel(
                 gate_i_of[r + 1] = input_gate(r + 1)
             if r + 2 < N_GROUPS:
                 quantise_h(r + 2)
-            if r < N_GROUPS:
-                use(GATE_F, r, f_T)
+            use(GATE_F, r, f_T)
             if r + 1 < N_GROUPS:
                 finish_input_gate(r + 1, gate_i_of[r + 1])
-        use(GATE_O, N_GROUPS - 1, o_T_of[N_GROUPS - 1])
+
+        last = N_GROUPS - 1
+        o_T_of[last] = squash(GATE_O, last)
+        use(GATE_O, last - 1, o_T_of[last - 1])
+        tanh_cell(last)
+        use(GATE_O, last, o_T_of[last])

@@ -24,7 +24,6 @@ CHUNKS = WIDTH // P
 GROUP_SLOTS = 4
 N_GROUPS = SLOTS // GROUP_SLOTS
 GROUP_COLS = GROUP_SLOTS * WIDTH
-HALF_COLS = GROUP_COLS // 2
 PASS_COLS = GROUP_SLOTS * P
 WORDS = WIDTH // 2
 W_X, W_H = 0, 1
@@ -264,11 +263,11 @@ def tile_rlstmcell_pb_kernel(
                     first = g * GROUP_COLS + s * WIDTH
                     nc.sync.dma_start(out=out_0[:, first : first + WIDTH], in_=product[:, cols])
             if gate == GATE_F:
-                for half, engine in enumerate((nc.vector, nc.gpsimd)):
-                    cols = slice(half * HALF_COLS, (half + 1) * HALF_COLS)
-                    engine.tensor_tensor(out=c_new[g][:, cols], in0=c_new[g][:, cols], in1=i_cand[g][:, cols], op=ADD)
-                    first = g * GROUP_COLS + half * HALF_COLS
-                    nc.sync.dma_start(out=out_1[:, first : first + HALF_COLS], in_=c_new[g][:, cols])
+                for s in range(GROUP_SLOTS):
+                    cols = slice(s * WIDTH, (s + 1) * WIDTH)
+                    nc.vector.tensor_tensor(out=c_new[g][:, cols], in0=c_new[g][:, cols], in1=i_cand[g][:, cols], op=ADD)
+                    first = g * GROUP_COLS + s * WIDTH
+                    nc.sync.dma_start(out=out_1[:, first : first + WIDTH], in_=c_new[g][:, cols])
 
         x_bank = t_banks.tile([P, WIDTH], FP32, tag="t_bank")
         nc.tensor.matmul_mx(

@@ -29,7 +29,11 @@ WORDS = WIDTH // 2
 W_X, W_H = 0, 1
 QUADS = 4
 PSUM_BANKS = 8
-EARLY_CANDS = 2
+POOL_SHARE = [[],[],[],[]]
+LOADS = "u0a x h0 u0b b R u1a K r k u1b h1 u2 h2 c0 u3 h3 c1 c2 c3"
+TU_COLS = 1024
+LEAD = 3
+EARLY_CANDS = 3
 
 FLOPS = 2 * WIDTH * GATES * WIDTH * (P + P * SLOTS)
 
@@ -109,25 +113,36 @@ def tile_rlstmcell_pb_kernel(
                     in_=scales[0, 4 * quad : 4 * quad + 4, :].bitcast(I32),
                 )
 
-        nc.sync.dma_start(out=x_sb[:], in_=inputs)
-        load_h(0)
-        load_c_upd(0)
-        nc.sync.dma_start(out=bias_rows[0 : GATES * CHUNKS, :], in_=bias.rearrange("(j p) -> j p", p=P))
-        nc.sync.dma_start(out=bias_row0[0:1, :], in_=bias[GATE_I * WIDTH : (GATE_I + 1) * WIDTH].unsqueeze(0))
-        nc.sync.dma_start(out=w_words[:, W_H, :].bitcast(I32), in_=recurrent_kernel_words[0].bitcast(I32))
-        nc.sync.dma_start(out=w_words[:, W_X, :].bitcast(I32), in_=kernel_words[0].bitcast(I32))
-        load_scales(W_H, recurrent_kernel_scales)
-        load_scales(W_X, kernel_scales)
-        load_c_upd(1)
-        load_h(1)
-        load_c_upd(2)
-        load_c(0)
-        load_c_upd(3)
-        load_h(2)
-        load_c(1)
-        load_h(3)
-        load_c(2)
-        load_c(3)
+        def load_part(tiles, rows, g, first_slot, n_slots):
+            a = first_slot * WIDTH
+            b = a + n_slots * WIDTH
+            nc.sync.dma_start(out=tiles[g][:, a:b], in_=rows[:, g * GROUP_COLS + a : g * GROUP_COLS + b])
+
+        def load_named(what):
+            kind = what[0]
+            if kind == "x":
+                nc.sync.dma_start(out=x_sb[:], in_=inputs)
+            elif kind == "b":
+                nc.sync.dma_start(out=bias_rows[0 : GATES * CHUNKS, :], in_=bias.rearrange("(j p) -> j p", p=P))
+                nc.sync.dma_start(out=bias_row0[0:1, :], in_=bias[GATE_I * WIDTH : (GATE_I + 1) * WIDTH].unsqueeze(0))
+            elif kind == "R":
+                nc.sync.dma_start(out=w_words[:, W_H, :].bitcast(I32), in_=recurrent_kernel_words[0].bitcast(I32))
+            elif kind == "K":
+                nc.sync.dma_start(out=w_words[:, W_X, :].bitcast(I32), in_=kernel_words[0].bitcast(I32))
+            elif kind == "r":
+                load_scales(W_H, recurrent_kernel_scales)
+            elif kind == "k":
+                load_scales(W_X, kernel_scales)
+            else:
+                tiles, rows = {"u": (u_sb, c_upd_rows), "h": (h_sb, h_state), "c": (c_sb, c_state)}[kind]
+                g = int(what[1])
+                if len(what) == 2:
+                    load_part(tiles, rows, g, 0, GROUP_SLOTS)
+                else:
+                    load_part(tiles, rows, g, 2 * (what[2] == "b"), 2)
+
+        for what in LOADS.split():
+            load_named(what)
 
         def turn_slots(rows, slot_list, grouped_words, repeat):
             turned = t_banks.tile([P, len(slot_list), 2, P], FP32, tag="t_bank")
@@ -180,7 +195,8 @@ def tile_rlstmcell_pb_kernel(
 
         def tanh_candidate(g):
             cand[g] = cands.tile([P, GROUP_COLS], FP32, name="cand")
-            nc.scalar.activation(out=cand[g][:], in_=u_sb[g][:], func=TANH)
+            for a in range(0, GROUP_COLS, TU_COLS):
+                nc.scalar.activation(out=cand[g][:, a : a + TU_COLS], in_=u_sb[g][:, a : a + TU_COLS], func=TANH)
 
         def tanh_cell(g):
             tanh_c[g] = work.tile([P, GROUP_COLS], FP32, name="tanh_c")
@@ -265,7 +281,8 @@ def tile_rlstmcell_pb_kernel(
             if gate == GATE_F:
                 for s in range(GROUP_SLOTS):
                     cols = slice(s * WIDTH, (s + 1) * WIDTH)
-                    nc.vector.tensor_tensor(out=c_new[g][:, cols], in0=c_new[g][:, cols], in1=i_cand[g][:, cols], op=ADD)
+                    engine = nc.gpsimd if s in POOL_SHARE[g] else nc.vector
+                    engine.tensor_tensor(out=c_new[g][:, cols], in0=c_new[g][:, cols], in1=i_cand[g][:, cols], op=ADD)
                     first = g * GROUP_COLS + s * WIDTH
                     nc.sync.dma_start(out=out_1[:, first : first + WIDTH], in_=c_new[g][:, cols])
 
@@ -286,8 +303,9 @@ def tile_rlstmcell_pb_kernel(
             tanh_candidate(g)
         gate_i_of[0] = input_gate(0)
         finish_input_gate(0, gate_i_of[0])
-        turn_h(1)
-        quantise_h(1)
+        for g in range(1, LEAD):
+            turn_h(g)
+            quantise_h(g)
 
         o_T_of = {}
         for r in range(N_GROUPS):
@@ -300,12 +318,12 @@ def tile_rlstmcell_pb_kernel(
                 tanh_candidate(r + EARLY_CANDS)
             if r >= 1:
                 tanh_cell(r - 1)
-            if r + 2 < N_GROUPS:
-                turn_h(r + 2)
+            if r + LEAD < N_GROUPS:
+                turn_h(r + LEAD)
             if r + 1 < N_GROUPS:
                 gate_i_of[r + 1] = input_gate(r + 1)
-            if r + 2 < N_GROUPS:
-                quantise_h(r + 2)
+            if r + LEAD < N_GROUPS:
+                quantise_h(r + LEAD)
             use(GATE_F, r, f_T)
             if r + 1 < N_GROUPS:
                 finish_input_gate(r + 1, gate_i_of[r + 1])

@@ -29,11 +29,9 @@ WORDS = WIDTH // 2
 W_X, W_H = 0, 1
 QUADS = 4
 PSUM_BANKS = 8
-POOL_SHARE = [[],[],[],[]]
-LOADS = "u0a x h0 u0b b R u1a K r k u1b h1 u2 h2 c0 u3 h3 c1 c2 c3"
-TU_COLS = 1024
-LEAD = 3
-EARLY_CANDS = 3
+POOL_COLS = 512
+TAIL_FROM = 3
+LOADS = "x h0a b u0a h0b K u0b k R u1a u1b r h1 u2 h2 c0 u3 h3 c1 c2 c3"
 
 FLOPS = 2 * WIDTH * GATES * WIDTH * (P + P * SLOTS)
 
@@ -60,7 +58,7 @@ def tile_rlstmcell_pb_kernel(
         consts = ctx.enter_context(tc.tile_pool(name="consts", bufs=1))
         loads = ctx.enter_context(tc.tile_pool(name="loads", bufs=1))
         stage = ctx.enter_context(tc.tile_pool(name="stage", bufs=2))
-        gates = ctx.enter_context(tc.tile_pool(name="gates", bufs=2 * CHUNKS))
+        gates = ctx.enter_context(tc.tile_pool(name="gates", bufs=3 * CHUNKS))
         work = ctx.enter_context(tc.tile_pool(name="work", bufs=2))
         cands = ctx.enter_context(tc.tile_pool(name="cands", bufs=N_GROUPS))
         z_banks = ctx.enter_context(tc.psum_pool(name="z_banks", bufs=PSUM_BANKS // 2))
@@ -78,6 +76,9 @@ def tile_rlstmcell_pb_kernel(
         ones = consts.tile([P, P], BF16)
         warm = consts.tile([P, 1], FP32)
         x_sb = consts.tile([P, WIDTH], BF16)
+        x_once = consts.tile([P, 4 * P], BF16, align_bytes=64)
+        x_codes1 = consts.tile([P, P], U32, align_bytes=64)
+        x_scales1 = consts.tile([P, P], U8, align_bytes=64)
         x_codes = consts.tile([P, PASS_COLS], U32, align_bytes=64)
         x_scales = consts.tile([P, PASS_COLS], U8, align_bytes=64)
         h_codes = consts.tile([P, N_GROUPS, PASS_COLS], U32, align_bytes=64)
@@ -90,21 +91,15 @@ def tile_rlstmcell_pb_kernel(
         nc.vector.memset(bias_row0[:], 0.0)
         nc.vector.memset(ones[:], 1.0)
         nc.vector.memset(w_scales[:].bitcast(I32), 0)
+        nc.vector.memset(x_scales1[:].bitcast(I32), 0)
         nc.vector.memset(warm[:], 0.0)
         make_identity(nc, ident[:])
         nc.scalar.activation(out=warm[:], in_=warm[:], func=SIGMOID)
 
-        def group_cols(g):
-            return slice(g * GROUP_COLS, (g + 1) * GROUP_COLS)
-
-        def load_h(g):
-            nc.sync.dma_start(out=h_sb[g][:], in_=h_state[:, group_cols(g)])
-
-        def load_c_upd(g):
-            nc.sync.dma_start(out=u_sb[g][:], in_=c_upd_rows[:, group_cols(g)])
-
-        def load_c(g):
-            nc.sync.dma_start(out=c_sb[g][:], in_=c_state[:, group_cols(g)])
+        def load(tiles, rows, g, first_slot=0, n_slots=GROUP_SLOTS):
+            a = first_slot * WIDTH
+            b = a + n_slots * WIDTH
+            nc.sync.dma_start(out=tiles[g][:, a:b], in_=rows[:, g * GROUP_COLS + a : g * GROUP_COLS + b])
 
         def load_scales(w, scales):
             for quad in range(QUADS):
@@ -112,11 +107,6 @@ def tile_rlstmcell_pb_kernel(
                     out=w_scales[32 * quad : 32 * quad + 4, w, :].bitcast(I32),
                     in_=scales[0, 4 * quad : 4 * quad + 4, :].bitcast(I32),
                 )
-
-        def load_part(tiles, rows, g, first_slot, n_slots):
-            a = first_slot * WIDTH
-            b = a + n_slots * WIDTH
-            nc.sync.dma_start(out=tiles[g][:, a:b], in_=rows[:, g * GROUP_COLS + a : g * GROUP_COLS + b])
 
         def load_named(what):
             kind = what[0]
@@ -137,9 +127,9 @@ def tile_rlstmcell_pb_kernel(
                 tiles, rows = {"u": (u_sb, c_upd_rows), "h": (h_sb, h_state), "c": (c_sb, c_state)}[kind]
                 g = int(what[1])
                 if len(what) == 2:
-                    load_part(tiles, rows, g, 0, GROUP_SLOTS)
+                    load(tiles, rows, g)
                 else:
-                    load_part(tiles, rows, g, 2 * (what[2] == "b"), 2)
+                    load(tiles, rows, g, 2 * (what[2] == "b"), 2)
 
         for what in LOADS.split():
             load_named(what)
@@ -175,28 +165,18 @@ def tile_rlstmcell_pb_kernel(
                 out=h_codes[:, g, :].bitcast(E4M3X4), scales=h_scales[:, g, :], in_=grouped_of[g][:]
             )
 
-        x_grouped, x_grouped_words = new_grouped()
-        turn_slots(x_sb[:].bitcast(FP32), [0], x_grouped_words, GROUP_SLOTS)
-        turn_h(0)
-        nc.vector.quantize_mx(out=x_codes[:].bitcast(E4M3X4), scales=x_scales[:], in_=x_grouped[:])
-        nc.vector.tensor_copy(out=bias_rows_f32[:], in_=bias_rows[:])
-        bias_bank = t_banks.tile([P, P], FP32, tag="t_bank")
-        nc.tensor.transpose(bias_bank[:], bias_rows_f32[:], ident[:])
-        quantise_h(0)
-        nc.vector.tensor_copy(out=bias_T[:], in_=bias_bank[:, 0 : GATES * CHUNKS])
-        spread_bank = t_banks.tile([P, WIDTH], FP32, tag="t_bank")
-        nc.tensor.matmul(out=spread_bank[:], lhsT=ones[:], rhs=bias_row0[:], start=True, stop=True)
-        nc.vector.tensor_copy(out=bias_i[:], in_=spread_bank[:])
-
         cand = {}
-        i_cand = {}
         c_new = {}
         tanh_c = {}
+        gate_i_of = {}
+        z_of = {}
+        T_of = {}
 
-        def tanh_candidate(g):
-            cand[g] = cands.tile([P, GROUP_COLS], FP32, name="cand")
-            for a in range(0, GROUP_COLS, TU_COLS):
-                nc.scalar.activation(out=cand[g][:, a : a + TU_COLS], in_=u_sb[g][:, a : a + TU_COLS], func=TANH)
+        def tanh_candidate(g, first_slot=0, n_slots=GROUP_SLOTS):
+            if first_slot == 0:
+                cand[g] = cands.tile([P, GROUP_COLS], FP32, name="cand")
+            cols = slice(first_slot * WIDTH, (first_slot + n_slots) * WIDTH)
+            nc.scalar.activation(out=cand[g][:, cols], in_=u_sb[g][:, cols], func=TANH)
 
         def tanh_cell(g):
             tanh_c[g] = work.tile([P, GROUP_COLS], FP32, name="tanh_c")
@@ -226,17 +206,18 @@ def tile_rlstmcell_pb_kernel(
                 nc.vector.tensor_tensor(
                     out=gate_i[:, s * WIDTH : (s + 1) * WIDTH], in0=bank[:], in1=x_part_i[:], op=ADD
                 )
-            return gate_i
+            gate_i_of[g] = gate_i
 
-        def finish_input_gate(g, gate_i):
-            nc.scalar.activation(out=gate_i[:], in_=gate_i[:], func=SIGMOID)
-            i_cand[g] = work.tile([P, GROUP_COLS], FP32, name="i_cand")
-            for s in range(GROUP_SLOTS):
-                cols = slice(s * WIDTH, (s + 1) * WIDTH)
-                nc.gpsimd.tensor_tensor(out=i_cand[g][:, cols], in0=gate_i[:, cols], in1=cand[g][:, cols], op=MULT)
+        def squash_i(g):
+            nc.scalar.activation(out=gate_i_of[g][:], in_=gate_i_of[g][:], func=SIGMOID)
 
-        def squash(gate, g):
-            gate_T = []
+        def times_candidate(g):
+            for a in range(0, GROUP_COLS, POOL_COLS):
+                cols = slice(a, a + POOL_COLS)
+                nc.gpsimd.tensor_tensor(out=cand[g][:, cols], in0=gate_i_of[g][:, cols], in1=cand[g][:, cols], op=MULT)
+
+        def fill(gate, g):
+            banks = []
             for j in range(CHUNKS):
                 chunk = gate * CHUNKS + j
                 z_T = z_banks.tile([P, PASS_COLS], FP32, name="z_T")
@@ -253,14 +234,22 @@ def tile_rlstmcell_pb_kernel(
                         start=(w == W_X),
                         stop=(w == W_H),
                     )
+                banks.append(z_T)
+            z_of[gate, g] = banks
+
+        def squash(gate, g):
+            gate_T = []
+            for j in range(CHUNKS):
+                chunk = gate * CHUNKS + j
                 squashed = gates.tile([P, PASS_COLS], FP32, name="squashed")
                 nc.scalar.activation(
-                    out=squashed[:], in_=z_T[:], func=SIGMOID, bias=bias_T[:, chunk : chunk + 1], scale=1.0
+                    out=squashed[:], in_=z_of[gate, g][j][:], func=SIGMOID, bias=bias_T[:, chunk : chunk + 1], scale=1.0
                 )
                 gate_T.append(squashed)
-            return gate_T
+            T_of[gate, g] = gate_T
 
-        def use(gate, g, gate_T):
+        def use(gate, g):
+            gate_T = T_of[gate, g]
             if gate == GATE_F:
                 c_new[g] = work.tile([P, GROUP_COLS], FP32, name="c_new")
                 product, partner = c_new[g], c_sb[g]
@@ -278,19 +267,43 @@ def tile_rlstmcell_pb_kernel(
                 if gate == GATE_O:
                     first = g * GROUP_COLS + s * WIDTH
                     nc.sync.dma_start(out=out_0[:, first : first + WIDTH], in_=product[:, cols])
-            if gate == GATE_F:
-                for s in range(GROUP_SLOTS):
-                    cols = slice(s * WIDTH, (s + 1) * WIDTH)
-                    engine = nc.gpsimd if s in POOL_SHARE[g] else nc.vector
-                    engine.tensor_tensor(out=c_new[g][:, cols], in0=c_new[g][:, cols], in1=i_cand[g][:, cols], op=ADD)
-                    first = g * GROUP_COLS + s * WIDTH
-                    nc.sync.dma_start(out=out_1[:, first : first + WIDTH], in_=c_new[g][:, cols])
 
+        def add_up(g, engine, first_slot, n_slots, width):
+            for a in range(first_slot * WIDTH, (first_slot + n_slots) * WIDTH, width):
+                cols = slice(a, a + width)
+                engine.tensor_tensor(out=c_new[g][:, cols], in0=c_new[g][:, cols], in1=cand[g][:, cols], op=ADD)
+                first = g * GROUP_COLS + a
+                nc.sync.dma_start(out=out_1[:, first : first + width], in_=c_new[g][:, cols])
+
+        def has(g):
+            return 0 <= g < N_GROUPS
+
+        turn_slots(x_sb[:].bitcast(FP32), [0], x_once[:].bitcast(FP32).rearrange("p (s b u) -> p s b u", s=1, b=P, u=2), 1)
+        turn_h(0)
+        nc.vector.quantize_mx(out=x_codes1[:].bitcast(E4M3X4), scales=x_scales1[:], in_=x_once[:])
+        nc.vector.tensor_copy(out=bias_rows_f32[:], in_=bias_rows[:])
+        bias_bank = t_banks.tile([P, P], FP32, tag="t_bank")
+        nc.tensor.transpose(bias_bank[:], bias_rows_f32[:], ident[:])
+        spread_bank = t_banks.tile([P, WIDTH], FP32, tag="t_bank")
+        nc.tensor.matmul(out=spread_bank[:], lhsT=ones[:], rhs=bias_row0[:], start=True, stop=True)
+        tanh_candidate(0, 0, 2)
+        tanh_candidate(0, 2, 2)
+        nc.scalar.copy(out=bias_i[:], in_=spread_bank[:])
+        quantise_h(0)
+        nc.vector.tensor_copy(
+            out=x_codes[:].bitcast(I32).rearrange("p (s b) -> p s b", s=GROUP_SLOTS),
+            in_=x_codes1[:].bitcast(I32).unsqueeze(1).to_broadcast([P, GROUP_SLOTS, P]),
+        )
+        nc.vector.tensor_copy(
+            out=x_scales[:].bitcast(I32).rearrange("p (s w) -> p s w", s=GROUP_SLOTS),
+            in_=x_scales1[:].bitcast(I32).unsqueeze(1).to_broadcast([P, GROUP_SLOTS, P // 4]),
+        )
+        nc.vector.tensor_copy(out=bias_T[:], in_=bias_bank[:, 0 : GATES * CHUNKS])
         x_bank = t_banks.tile([P, WIDTH], FP32, tag="t_bank")
         nc.tensor.matmul_mx(
             out=x_bank[:],
-            lhsT=x_codes[:, 0:P].bitcast(E4M3X4),
-            lhsT_scale=x_scales[:, 0:P],
+            lhsT=x_codes1[:].bitcast(E4M3X4),
+            lhsT_scale=x_scales1[:],
             rhs=gate_words(W_X, GATE_I),
             rhs_scale=gate_scales(W_X, GATE_I),
             start=True,
@@ -298,38 +311,35 @@ def tile_rlstmcell_pb_kernel(
         )
         nc.vector.tensor_tensor(out=x_part_i[:], in0=x_bank[:], in1=bias_i[:], op=ADD)
 
-        gate_i_of = {}
-        for g in range(EARLY_CANDS):
-            tanh_candidate(g)
-        gate_i_of[0] = input_gate(0)
-        finish_input_gate(0, gate_i_of[0])
-        for g in range(1, LEAD):
-            turn_h(g)
-            quantise_h(g)
-
-        o_T_of = {}
-        for r in range(N_GROUPS):
-            f_T = squash(GATE_F, r)
-            if r >= 2:
-                use(GATE_O, r - 2, o_T_of[r - 2])
-            if r >= 1:
-                o_T_of[r - 1] = squash(GATE_O, r - 1)
-            if r + EARLY_CANDS < N_GROUPS:
-                tanh_candidate(r + EARLY_CANDS)
-            if r >= 1:
+        for r in range(-2, N_GROUPS + 2):
+            early_o = r >= TAIL_FROM
+            if early_o and has(r - 2):
+                use(GATE_O, r - 2)
+            if has(r - 1):
+                fill(GATE_O, r - 1)
+            if has(r):
+                squash(GATE_F, r)
+            if has(r - 1):
+                squash(GATE_O, r - 1)
+            if 1 <= r + 2 < N_GROUPS:
+                tanh_candidate(r + 2, 2, 2)
+                turn_h(r + 2)
+            if not early_o and has(r - 2):
+                use(GATE_O, r - 2)
+            if has(r):
+                use(GATE_F, r)
+            if 1 <= r + 2 < N_GROUPS:
+                quantise_h(r + 2)
+            if has(r):
+                add_up(r, nc.vector, 0, GROUP_SLOTS, WIDTH)
+            if 1 <= r + 3 < N_GROUPS:
+                tanh_candidate(r + 3, 0, 2)
+            if has(r + 1):
+                fill(GATE_F, r + 1)
+            if has(r + 2):
+                input_gate(r + 2)
+            if has(r + 1):
+                squash_i(r + 1)
+                times_candidate(r + 1)
+            if has(r - 1):
                 tanh_cell(r - 1)
-            if r + LEAD < N_GROUPS:
-                turn_h(r + LEAD)
-            if r + 1 < N_GROUPS:
-                gate_i_of[r + 1] = input_gate(r + 1)
-            if r + LEAD < N_GROUPS:
-                quantise_h(r + LEAD)
-            use(GATE_F, r, f_T)
-            if r + 1 < N_GROUPS:
-                finish_input_gate(r + 1, gate_i_of[r + 1])
-
-        last = N_GROUPS - 1
-        o_T_of[last] = squash(GATE_O, last)
-        use(GATE_O, last - 1, o_T_of[last - 1])
-        tanh_cell(last)
-        use(GATE_O, last, o_T_of[last])

@@ -74,6 +74,7 @@ def tile_rlstmcell_pb_kernel(
         x_part_i = consts.tile([P, WIDTH], FP32)
         bias_row0 = consts.tile([P, WIDTH], BF16)
         ones = consts.tile([P, P], BF16)
+        zeros = consts.tile([P, WIDTH], BF16)
         warm = consts.tile([P, 1], FP32)
         x_sb = consts.tile([P, WIDTH], BF16)
         x_once = consts.tile([P, 4 * P], BF16, align_bytes=64)
@@ -90,6 +91,7 @@ def tile_rlstmcell_pb_kernel(
         nc.vector.memset(bias_rows[:], 0.0)
         nc.vector.memset(bias_row0[:], 0.0)
         nc.vector.memset(ones[:], 1.0)
+        nc.vector.memset(zeros[:], 0.0)
         nc.vector.memset(w_scales[:].bitcast(I32), 0)
         nc.vector.memset(x_scales1[:].bitcast(I32), 0)
         nc.vector.memset(warm[:], 0.0)
@@ -248,7 +250,7 @@ def tile_rlstmcell_pb_kernel(
                 gate_T.append(squashed)
             T_of[gate, g] = gate_T
 
-        def use(gate, g):
+        def use(gate, g, run_starts_here=False):
             gate_T = T_of[gate, g]
             if gate == GATE_F:
                 c_new[g] = work.tile([P, GROUP_COLS], FP32, name="c_new")
@@ -259,6 +261,8 @@ def tile_rlstmcell_pb_kernel(
             for s in range(GROUP_SLOTS):
                 cols = slice(s * WIDTH, (s + 1) * WIDTH)
                 bank = t_banks.tile([P, WIDTH], FP32, tag="t_bank")
+                if s % 2 == 0 and not (s == 0 and run_starts_here):
+                    nc.tensor.matmul(out=bank[:], lhsT=ones[:], rhs=zeros[:], start=True, stop=True)
                 for j in range(CHUNKS):
                     nc.tensor.transpose(
                         bank[:, j * P : (j + 1) * P], gate_T[j][:, s * P : (s + 1) * P], ident[:]
@@ -314,7 +318,7 @@ def tile_rlstmcell_pb_kernel(
         for r in range(-2, N_GROUPS + 2):
             early_o = r >= TAIL_FROM
             if early_o and has(r - 2):
-                use(GATE_O, r - 2)
+                use(GATE_O, r - 2, True)
             if has(r - 1):
                 fill(GATE_O, r - 1)
             if has(r):
@@ -324,10 +328,11 @@ def tile_rlstmcell_pb_kernel(
             if 1 <= r + 2 < N_GROUPS:
                 tanh_candidate(r + 2, 2, 2)
                 turn_h(r + 2)
+            h_turned = 1 <= r + 2 < N_GROUPS
             if not early_o and has(r - 2):
-                use(GATE_O, r - 2)
+                use(GATE_O, r - 2, not h_turned)
             if has(r):
-                use(GATE_F, r)
+                use(GATE_F, r, early_o or not (h_turned or has(r - 2)))
             if 1 <= r + 2 < N_GROUPS:
                 quantise_h(r + 2)
             if has(r):

@@ -29,26 +29,13 @@ WORDS = WIDTH // 2
 W_X, W_H = 0, 1
 QUADS = 4
 PSUM_BANKS = 8
-POOL_COLS = 512
-TAIL_FROM = 3
-LOADS = "x h0a b u0a h0b K u0b k R u1a u1b r h1 u2 h2 c0 u3 h3 c1 c2 c3"
+LOADS = "u0a x h0a u0b h0b b K k u1a R u1b r u2 h1 h2 u3 c0 h3 c1 c2 c3"
 
 FLOPS = 2 * WIDTH * GATES * WIDTH * (P + P * SLOTS)
 
 
 def tile_rlstmcell_pb_kernel(
-    tc,
-    inputs,
-    h_state,
-    c_state,
-    c_upd,
-    kernel_words,
-    kernel_scales,
-    recurrent_kernel_words,
-    recurrent_kernel_scales,
-    bias,
-    out_0,
-    out_1,
+    tc, inputs, h_state, c_state, c_upd, kernel_words, kernel_scales, recurrent_kernel_words, recurrent_kernel_scales, bias, out_0, out_1,
 ):
     nc = tc.nc
     c_upd_rows = c_upd.rearrange("b s d -> b (s d)")
@@ -57,12 +44,12 @@ def tile_rlstmcell_pb_kernel(
         ctx.enter_context(tc.manual_schedule())
         consts = ctx.enter_context(tc.tile_pool(name="consts", bufs=1))
         loads = ctx.enter_context(tc.tile_pool(name="loads", bufs=1))
-        stage = ctx.enter_context(tc.tile_pool(name="stage", bufs=2))
-        gates = ctx.enter_context(tc.tile_pool(name="gates", bufs=3 * CHUNKS))
-        work = ctx.enter_context(tc.tile_pool(name="work", bufs=2))
-        cands = ctx.enter_context(tc.tile_pool(name="cands", bufs=N_GROUPS))
-        z_banks = ctx.enter_context(tc.psum_pool(name="z_banks", bufs=PSUM_BANKS // 2))
-        t_banks = ctx.enter_context(tc.psum_pool(name="t_banks", bufs=PSUM_BANKS // 2))
+        stage = ctx.enter_context(tc.tile_pool(name="stage", bufs=3))
+        gates = ctx.enter_context(tc.tile_pool(name="gates", bufs=12))
+        work = ctx.enter_context(tc.tile_pool(name="work", bufs=6))
+        longer = ctx.enter_context(tc.tile_pool(name="longer", bufs=8))
+        z_banks = ctx.enter_context(tc.psum_pool(name="z_banks", bufs=4))
+        t_banks = ctx.enter_context(tc.psum_pool(name="t_banks", bufs=4))
 
         ident = consts.tile([P, P], FP32)
         w_words = consts.tile([P, 2, 2 * GATES * WIDTH], U8, align_bytes=64)
@@ -88,15 +75,15 @@ def tile_rlstmcell_pb_kernel(
         c_sb = [loads.tile([P, GROUP_COLS], BF16, name="c_sb%d" % g) for g in range(N_GROUPS)]
         u_sb = [loads.tile([P, GROUP_COLS], BF16, name="u_sb%d" % g) for g in range(N_GROUPS)]
 
+        nc.vector.memset(warm[:], 0.0)
+        nc.scalar.activation(out=warm[:], in_=warm[:], func=SIGMOID)
         nc.vector.memset(bias_rows[:], 0.0)
         nc.vector.memset(bias_row0[:], 0.0)
         nc.vector.memset(ones[:], 1.0)
         nc.vector.memset(zeros[:], 0.0)
         nc.vector.memset(w_scales[:].bitcast(I32), 0)
         nc.vector.memset(x_scales1[:].bitcast(I32), 0)
-        nc.vector.memset(warm[:], 0.0)
         make_identity(nc, ident[:])
-        nc.scalar.activation(out=warm[:], in_=warm[:], func=SIGMOID)
 
         def load(tiles, rows, g, first_slot=0, n_slots=GROUP_SLOTS):
             a = first_slot * WIDTH
@@ -133,58 +120,49 @@ def tile_rlstmcell_pb_kernel(
                 else:
                     load(tiles, rows, g, 2 * (what[2] == "b"), 2)
 
+
         for what in LOADS.split():
             load_named(what)
 
-        def turn_slots(rows, slot_list, grouped_words, repeat):
-            turned = t_banks.tile([P, len(slot_list), 2, P], FP32, tag="t_bank")
-            for n, s in enumerate(slot_list):
-                for u in range(2):
-                    nc.tensor.transpose(
-                        turned[:, n, u, :], rows[:, s * WORDS + u : (s + 1) * WORDS : 2], ident[:]
-                    )
-            by_row = turned[:].rearrange("p s u b -> p s b u")
-            if repeat > 1:
-                by_row = by_row.to_broadcast([P, repeat, P, 2])
-            nc.vector.tensor_copy(out=grouped_words, in_=by_row)
+        cand = [consts.tile([P, WIDTH], FP32, name="cand%d" % s) for s in range(SLOTS)]
+        c_new, tanh_c, gate_i_of, z_of, T_of, grouped_of = {}, {}, {}, {}, {}, {}
 
-        def new_grouped():
-            grouped = stage.tile([P, 4 * PASS_COLS], BF16, name="grouped", align_bytes=64)
-            words = grouped[:].bitcast(FP32).rearrange("p (s b u) -> p s b u", s=GROUP_SLOTS, b=P, u=2)
-            return grouped, words
+        def slot_cols(s):
+            return slice((s % GROUP_SLOTS) * WIDTH, (s % GROUP_SLOTS + 1) * WIDTH)
 
-        grouped_of = {}
+        def turn(rows, s, grouped):
+            bank = t_banks.tile([P, 2, P], FP32, tag="t_bank")
+            for u in range(2):
+                nc.tensor.transpose(bank[:, u, :], rows[:, s * WORDS + u : (s + 1) * WORDS : 2], ident[:])
+            return bank, grouped
 
-        def turn_h(g):
-            grouped, words = new_grouped()
-            rows = h_sb[g][:].bitcast(FP32)
-            turn_slots(rows, [0, 1], words[:, 0:2], 1)
-            turn_slots(rows, [2, 3], words[:, 2:4], 1)
-            grouped_of[g] = grouped
-
-        def quantise_h(g):
-            nc.vector.quantize_mx(
-                out=h_codes[:, g, :].bitcast(E4M3X4), scales=h_scales[:, g, :], in_=grouped_of[g][:]
+        def unturn(pair):
+            bank, grouped = pair
+            nc.vector.tensor_copy(
+                out=grouped[:].bitcast(FP32).rearrange("p (b u) -> p b u", b=P, u=2), in_=bank[:].rearrange("p u b -> p b u")
             )
 
-        cand = {}
-        c_new = {}
-        tanh_c = {}
-        gate_i_of = {}
-        z_of = {}
-        T_of = {}
+        def turn_h(p):
+            rows = h_sb[p // 2][:].bitcast(FP32)
+            bank = t_banks.tile([P, 2, 2, P], FP32, tag="t_bank")
+            for n in range(2):
+                s = 2 * (p % 2) + n
+                for u in range(2):
+                    nc.tensor.transpose(bank[:, n, u, :], rows[:, s * WORDS + u : (s + 1) * WORDS : 2], ident[:])
+            grouped_of[p] = bank
 
-        def tanh_candidate(g, first_slot=0, n_slots=GROUP_SLOTS):
-            if first_slot == 0:
-                cand[g] = cands.tile([P, GROUP_COLS], FP32, name="cand")
-            cols = slice(first_slot * WIDTH, (first_slot + n_slots) * WIDTH)
-            nc.scalar.activation(out=cand[g][:, cols], in_=u_sb[g][:, cols], func=TANH)
+        def copy_h(p):
+            grouped = stage.tile([P, 2 * 4 * P], BF16, name="grouped", align_bytes=64)
+            nc.vector.tensor_copy(
+                out=grouped[:].bitcast(FP32).rearrange("p (s b u) -> p s b u", s=2, b=P, u=2), in_=grouped_of[p][:].rearrange("p s u b -> p s b u")
+            )
+            grouped_of[p] = grouped
 
-        def tanh_cell(g):
-            tanh_c[g] = work.tile([P, GROUP_COLS], FP32, name="tanh_c")
-            for s in range(GROUP_SLOTS):
-                cols = slice(s * WIDTH, (s + 1) * WIDTH)
-                nc.scalar.activation(out=tanh_c[g][:, cols], in_=c_new[g][:, cols], func=TANH)
+        def quantise_h(p):
+            g, j = p // 2, p % 2
+            nc.vector.quantize_mx(
+                out=h_codes[:, g, 2 * j * P : 2 * (j + 1) * P].bitcast(E4M3X4), scales=h_scales[:, g, 2 * j * P : 2 * (j + 1) * P], in_=grouped_of[p][:]
+            )
 
         def gate_words(w, gate):
             return w_words[:, w, 2 * WIDTH * gate : 2 * WIDTH * (gate + 1)].bitcast(E2M1X4)
@@ -192,159 +170,251 @@ def tile_rlstmcell_pb_kernel(
         def gate_scales(w, gate):
             return w_scales[:, w, WIDTH * gate : WIDTH * (gate + 1)]
 
-        def input_gate(g):
-            gate_i = work.tile([P, GROUP_COLS], FP32, name="gate_i")
-            for s in range(GROUP_SLOTS):
-                bank = t_banks.tile([P, WIDTH], FP32, tag="t_bank")
+        def tanh_candidate(s, n=1):
+            for k in range(s, s + n):
+                nc.scalar.activation(out=cand[k][:], in_=u_sb[k // GROUP_SLOTS][:, slot_cols(k)], func=TANH)
+
+        i_bank = {}
+
+        def fill_i(s):
+            g, j = s // GROUP_SLOTS, s % GROUP_SLOTS
+            bank = t_banks.tile([P, WIDTH], FP32, tag="t_bank")
+            nc.tensor.matmul_mx(
+                out=bank[:],
+                lhsT=h_codes[:, g, j * P : (j + 1) * P].bitcast(E4M3X4),
+                lhsT_scale=h_scales[:, g, j * P : (j + 1) * P],
+                rhs=gate_words(W_H, GATE_I),
+                rhs_scale=gate_scales(W_H, GATE_I),
+                start=True,
+                stop=True,
+            )
+            i_bank[s] = bank
+
+        def add_i(s):
+            gate_i = work.tile([P, WIDTH], FP32, name="gate_i")
+            nc.vector.tensor_tensor(out=gate_i[:], in0=i_bank[s][:], in1=x_part_i[:], op=ADD)
+            gate_i_of[s] = gate_i
+
+        def squash_i(s):
+            nc.scalar.activation(out=gate_i_of[s][:], in_=gate_i_of[s][:], func=SIGMOID)
+
+        def times_candidate(s):
+            nc.gpsimd.tensor_tensor(out=cand[s][:], in0=gate_i_of[s][:], in1=cand[s][:], op=MULT)
+
+        def fill(gate, g, j):
+            chunk = gate * CHUNKS + j
+            z_T = z_banks.tile([P, PASS_COLS], FP32, name="z_T")
+            for w, codes, scales in (
+                (W_X, x_codes[:], x_scales[:]),
+                (W_H, h_codes[:, g, :], h_scales[:, g, :]),
+            ):
                 nc.tensor.matmul_mx(
-                    out=bank[:],
-                    lhsT=h_codes[:, g, s * P : (s + 1) * P].bitcast(E4M3X4),
-                    lhsT_scale=h_scales[:, g, s * P : (s + 1) * P],
-                    rhs=gate_words(W_H, GATE_I),
-                    rhs_scale=gate_scales(W_H, GATE_I),
-                    start=True,
-                    stop=True,
+                    out=z_T[:],
+                    lhsT=w_words[:, w, 2 * P * chunk : 2 * P * (chunk + 1)].bitcast(E2M1X4),
+                    lhsT_scale=w_scales[:, w, P * chunk : P * (chunk + 1)],
+                    rhs=codes.bitcast(E4M3X4),
+                    rhs_scale=scales,
+                    start=(w == W_X),
+                    stop=(w == W_H),
                 )
-                nc.vector.tensor_tensor(
-                    out=gate_i[:, s * WIDTH : (s + 1) * WIDTH], in0=bank[:], in1=x_part_i[:], op=ADD
-                )
-            gate_i_of[g] = gate_i
+            z_of[gate, g, j] = z_T
 
-        def squash_i(g):
-            nc.scalar.activation(out=gate_i_of[g][:], in_=gate_i_of[g][:], func=SIGMOID)
+        def squash(gate, g, j):
+            chunk = gate * CHUNKS + j
+            squashed = gates.tile([P, PASS_COLS], FP32, name="squashed")
+            nc.scalar.activation(
+                out=squashed[:], in_=z_of[gate, g, j][:], func=SIGMOID, bias=bias_T[:, chunk : chunk + 1], scale=1.0
+            )
+            T_of[gate, g, j] = squashed
 
-        def times_candidate(g):
-            for a in range(0, GROUP_COLS, POOL_COLS):
-                cols = slice(a, a + POOL_COLS)
-                nc.gpsimd.tensor_tensor(out=cand[g][:, cols], in0=gate_i_of[g][:, cols], in1=cand[g][:, cols], op=MULT)
+        back = {}
+        late = set()
 
-        def fill(gate, g):
-            banks = []
+        def turn_back(gate, s):
+            g, q = s // GROUP_SLOTS, s % GROUP_SLOTS
+            bank = t_banks.tile([P, WIDTH], FP32, tag="t_bank")
             for j in range(CHUNKS):
-                chunk = gate * CHUNKS + j
-                z_T = z_banks.tile([P, PASS_COLS], FP32, name="z_T")
-                for w, codes, scales in (
-                    (W_X, x_codes[:], x_scales[:]),
-                    (W_H, h_codes[:, g, :], h_scales[:, g, :]),
-                ):
-                    nc.tensor.matmul_mx(
-                        out=z_T[:],
-                        lhsT=w_words[:, w, 2 * P * chunk : 2 * P * (chunk + 1)].bitcast(E2M1X4),
-                        lhsT_scale=w_scales[:, w, P * chunk : P * (chunk + 1)],
-                        rhs=codes.bitcast(E4M3X4),
-                        rhs_scale=scales,
-                        start=(w == W_X),
-                        stop=(w == W_H),
-                    )
-                banks.append(z_T)
-            z_of[gate, g] = banks
+                nc.tensor.transpose(bank[:, j * P : (j + 1) * P], T_of[gate, g, j][:, q * P : (q + 1) * P], ident[:])
+            back[gate, s] = bank
 
-        def squash(gate, g):
-            gate_T = []
-            for j in range(CHUNKS):
-                chunk = gate * CHUNKS + j
-                squashed = gates.tile([P, PASS_COLS], FP32, name="squashed")
-                nc.scalar.activation(
-                    out=squashed[:], in_=z_of[gate, g][j][:], func=SIGMOID, bias=bias_T[:, chunk : chunk + 1], scale=1.0
-                )
-                gate_T.append(squashed)
-            T_of[gate, g] = gate_T
-
-        def use(gate, g, run_starts_here=False):
-            gate_T = T_of[gate, g]
+        def product(gate, s):
+            g = s // GROUP_SLOTS
             if gate == GATE_F:
-                c_new[g] = work.tile([P, GROUP_COLS], FP32, name="c_new")
-                product, partner = c_new[g], c_sb[g]
+                c_new[s] = longer.tile([P, WIDTH], FP32, name="c_new")
+                nc.vector.tensor_tensor(out=c_new[s][:], in0=back[gate, s][:], in1=c_sb[g][:, slot_cols(s)], op=MULT)
             else:
-                product = work.tile([P, GROUP_COLS], FP32, name="h_new")
-                partner = tanh_c[g]
-            for s in range(GROUP_SLOTS):
-                cols = slice(s * WIDTH, (s + 1) * WIDTH)
-                bank = t_banks.tile([P, WIDTH], FP32, tag="t_bank")
-                if s % 2 == 0 and not (s == 0 and run_starts_here):
-                    nc.tensor.matmul(out=bank[:], lhsT=ones[:], rhs=zeros[:], start=True, stop=True)
-                for j in range(CHUNKS):
-                    nc.tensor.transpose(
-                        bank[:, j * P : (j + 1) * P], gate_T[j][:, s * P : (s + 1) * P], ident[:]
+                h_new = work.tile([P, WIDTH], FP32, name="h_new")
+                width = WIDTH // 2 if s == SLOTS - 1 else WIDTH
+                for b in range(0, WIDTH, width):
+                    nc.vector.tensor_tensor(
+                        out=h_new[:, b : b + width], in0=back[gate, s][:, b : b + width], in1=tanh_c[s][:, b : b + width], op=MULT
                     )
-                nc.vector.tensor_tensor(out=product[:, cols], in0=bank[:], in1=partner[:, cols], op=MULT)
-                if gate == GATE_O:
-                    first = g * GROUP_COLS + s * WIDTH
-                    nc.sync.dma_start(out=out_0[:, first : first + WIDTH], in_=product[:, cols])
+                    nc.sync.dma_start(out=out_0[:, s * WIDTH + b : s * WIDTH + b + width], in_=h_new[:, b : b + width])
 
-        def add_up(g, engine, first_slot, n_slots, width):
-            for a in range(first_slot * WIDTH, (first_slot + n_slots) * WIDTH, width):
-                cols = slice(a, a + width)
-                engine.tensor_tensor(out=c_new[g][:, cols], in0=c_new[g][:, cols], in1=cand[g][:, cols], op=ADD)
-                first = g * GROUP_COLS + a
-                nc.sync.dma_start(out=out_1[:, first : first + width], in_=c_new[g][:, cols])
+        def add_up(s, engine):
+            engine.tensor_tensor(out=c_new[s][:], in0=c_new[s][:], in1=cand[s][:], op=ADD)
+            if engine is nc.vector:
+                nc.sync.dma_start(out=out_1[:, s * WIDTH : (s + 1) * WIDTH], in_=c_new[s][:])
+            else:
+                late.add(s)
+
+        def tanh_cell(s):
+            tanh_c[s] = longer.tile([P, WIDTH], FP32, name="tanh_c")
+            nc.scalar.activation(out=tanh_c[s][:], in_=c_new[s][:], func=TANH)
+            if s in late:
+                nc.sync.dma_start(out=out_1[:, s * WIDTH : (s + 1) * WIDTH], in_=c_new[s][:])
+
+
+        def turn_x():
+            grouped_of["x"] = turn(x_sb[:].bitcast(FP32), 0, x_once)
+        def copy_x():
+            unturn(grouped_of["x"])
+        def quantise_x():
+            nc.vector.quantize_mx(out=x_codes1[:].bitcast(E4M3X4), scales=x_scales1[:], in_=x_once[:])
+        hold = {}
+        def bias_pe():
+            nc.vector.tensor_copy(out=bias_rows_f32[:], in_=bias_rows[:])
+            hold["b"] = t_banks.tile([P, P], FP32, name="bias_bank", tag="t_bank")
+            nc.tensor.transpose(hold["b"][:], bias_rows_f32[:], ident[:])
+            hold["s"] = t_banks.tile([P, WIDTH], FP32, name="spread_bank", tag="t_bank")
+            nc.tensor.matmul(out=hold["s"][:], lhsT=ones[:], rhs=bias_row0[:], start=True, stop=True)
+        def bias_v():
+            nc.vector.tensor_copy(out=bias_T[:], in_=hold["b"][:, 0 : GATES * CHUNKS])
+        def bias_a():
+            nc.vector.tensor_copy(out=bias_i[:], in_=hold["s"][:])
+        def x_pe():
+            hold["x"] = t_banks.tile([P, WIDTH], FP32, name="x_bank", tag="t_bank")
+            nc.tensor.matmul_mx(
+                out=hold["x"][:], lhsT=x_codes1[:].bitcast(E4M3X4), lhsT_scale=x_scales1[:],
+                rhs=gate_words(W_X, GATE_I), rhs_scale=gate_scales(W_X, GATE_I), start=True, stop=True,
+            )
+        def x_v():
+            nc.vector.tensor_tensor(out=x_part_i[:], in0=hold["x"][:], in1=bias_i[:], op=ADD)
+        def spread_x():
+            nc.vector.tensor_copy(
+                out=x_codes[:].bitcast(I32).rearrange("p (s b) -> p s b", s=GROUP_SLOTS),
+                in_=x_codes1[:].bitcast(I32).unsqueeze(1).to_broadcast([P, GROUP_SLOTS, P]),
+            )
+            nc.vector.tensor_copy(
+                out=x_scales[:].bitcast(I32).rearrange("p (s w) -> p s w", s=GROUP_SLOTS),
+                in_=x_scales1[:].bitcast(I32).unsqueeze(1).to_broadcast([P, GROUP_SLOTS, P // 4]),
+            )
 
         def has(g):
             return 0 <= g < N_GROUPS
+        def slots(a, n):
+            return [s for s in range(a, a + n) if 0 <= s < SLOTS]
+        def pairs(a, n):
+            return [p for p in range(a, a + n) if 0 <= p < SLOTS // 2]
+        def each(fn, what):
+            for w in what:
+                fn(w)
+        def both(a, b, what):
+            for w in what:
+                a(w)
+                b(w)
+        def zf(gate, g):
+            for j in range(CHUNKS):
+                fill(gate, g, j)
+        def sq(gate, g, j0=0, n=4):
+            for j in range(j0, j0 + n):
+                squash(gate, g, j)
+        def tt(gate, g):
+            for s in slots(4 * g, 4):
+                turn_back(gate, s)
+        def pr(gate, g):
+            for s in slots(4 * g, 4):
+                product(gate, s)
+        def si(s):
+            squash_i(s)
+            times_candidate(s)
+        def su(s):
+            add_up(s, nc.gpsimd if s % 2 == 1 else nc.vector)
+        def prsu(g):
+            a = 4 * g
+            product(GATE_F, a); product(GATE_F, a + 1)
+            su(a + 1); su(a)
+            product(GATE_F, a + 2); product(GATE_F, a + 3)
+            su(a + 3); su(a + 2)
+        def tu(s):
+            tanh_candidate(s)
+        def tc_(g):
+            for s in slots(4 * g, 4):
+                tanh_cell(s)
 
-        turn_slots(x_sb[:].bitcast(FP32), [0], x_once[:].bitcast(FP32).rearrange("p (s b u) -> p s b u", s=1, b=P, u=2), 1)
-        turn_h(0)
-        nc.vector.quantize_mx(out=x_codes1[:].bitcast(E4M3X4), scales=x_scales1[:], in_=x_once[:])
-        nc.vector.tensor_copy(out=bias_rows_f32[:], in_=bias_rows[:])
-        bias_bank = t_banks.tile([P, P], FP32, tag="t_bank")
-        nc.tensor.transpose(bias_bank[:], bias_rows_f32[:], ident[:])
-        spread_bank = t_banks.tile([P, WIDTH], FP32, tag="t_bank")
-        nc.tensor.matmul(out=spread_bank[:], lhsT=ones[:], rhs=bias_row0[:], start=True, stop=True)
-        tanh_candidate(0, 0, 2)
-        tanh_candidate(0, 2, 2)
-        nc.scalar.copy(out=bias_i[:], in_=spread_bank[:])
-        quantise_h(0)
-        nc.vector.tensor_copy(
-            out=x_codes[:].bitcast(I32).rearrange("p (s b) -> p s b", s=GROUP_SLOTS),
-            in_=x_codes1[:].bitcast(I32).unsqueeze(1).to_broadcast([P, GROUP_SLOTS, P]),
-        )
-        nc.vector.tensor_copy(
-            out=x_scales[:].bitcast(I32).rearrange("p (s w) -> p s w", s=GROUP_SLOTS),
-            in_=x_scales1[:].bitcast(I32).unsqueeze(1).to_broadcast([P, GROUP_SLOTS, P // 4]),
-        )
-        nc.vector.tensor_copy(out=bias_T[:], in_=bias_bank[:, 0 : GATES * CHUNKS])
-        x_bank = t_banks.tile([P, WIDTH], FP32, tag="t_bank")
-        nc.tensor.matmul_mx(
-            out=x_bank[:],
-            lhsT=x_codes1[:].bitcast(E4M3X4),
-            lhsT_scale=x_scales1[:],
-            rhs=gate_words(W_X, GATE_I),
-            rhs_scale=gate_scales(W_X, GATE_I),
-            start=True,
-            stop=True,
-        )
-        nc.vector.tensor_tensor(out=x_part_i[:], in0=x_bank[:], in1=bias_i[:], op=ADD)
 
-        for r in range(-2, N_GROUPS + 2):
-            early_o = r >= TAIL_FROM
-            if early_o and has(r - 2):
-                use(GATE_O, r - 2, True)
-            if has(r - 1):
-                fill(GATE_O, r - 1)
-            if has(r):
-                squash(GATE_F, r)
-            if has(r - 1):
-                squash(GATE_O, r - 1)
-            if 1 <= r + 2 < N_GROUPS:
-                tanh_candidate(r + 2, 2, 2)
-                turn_h(r + 2)
-            h_turned = 1 <= r + 2 < N_GROUPS
-            if not early_o and has(r - 2):
-                use(GATE_O, r - 2, not h_turned)
-            if has(r):
-                use(GATE_F, r, early_o or not (h_turned or has(r - 2)))
-            if 1 <= r + 2 < N_GROUPS:
-                quantise_h(r + 2)
-            if has(r):
-                add_up(r, nc.vector, 0, GROUP_SLOTS, WIDTH)
-            if 1 <= r + 3 < N_GROUPS:
-                tanh_candidate(r + 3, 0, 2)
-            if has(r + 1):
-                fill(GATE_F, r + 1)
-            if has(r + 2):
-                input_gate(r + 2)
-            if has(r + 1):
-                squash_i(r + 1)
-                times_candidate(r + 1)
-            if has(r - 1):
-                tanh_cell(r - 1)
+        turn_x(); copy_x(); turn_h(0); turn_h(1); quantise_x(); copy_h(0); copy_h(1)
+        bias_pe(); spread_x(); quantise_h(0); quantise_h(1); x_pe(); bias_v(); bias_a(); x_v()
+        done = [0]
+        def more(n):
+            for s in slots(done[0], n):
+                tu(s)
+            done[0] += n
+        more(10)
+        def sum_g(g, engine):
+            for s in slots(4 * g, 4):
+                if (engine is nc.gpsimd) == (s % 4 == 3 and s < 12):
+                    add_up(s, engine)
+        def H(p):
+            for q in pairs(p, 1):
+                turn_h(q); copy_h(q); quantise_h(q)
+        def I(s):
+            for q in slots(s, 2):
+                fill_i(q)
+            for q in slots(s, 2):
+                add_i(q)
+        def SI(s):
+            each(si, slots(s, 2))
+        def TC(s):
+            if s >= 0:
+                tanh_cell(s)
+            else:
+                more(1)
+        H(2) if 0 else None
+
+        for g in range(N_GROUPS):
+
+            a = 4 * g
+            fill(GATE_F, g, 0)
+            fill_i(a + 0)
+            fill_i(a + 1)
+            fill(GATE_F, g, 1)
+            fill(GATE_F, g, 2)
+            fill(GATE_F, g, 3)
+            fill_i(a + 2)
+            fill_i(a + 3)
+
+            each(add_i, slots(a, 2))
+            if has(g - 1):
+                sum_g(g - 1, nc.vector)
+            each(add_i, slots(a + 2, 2))
+            sq(GATE_F, g)
+            each(turn_h, pairs(2 * g + 2, 2)); each(copy_h, pairs(2 * g + 2, 2)); each(quantise_h, pairs(2 * g + 2, 2))
+            more(1)
+            for j in range(0, 4, 2):
+                each(si, slots(a + j, 2))
+                if g > 0:
+                    each(tanh_cell, slots(a - 4 + j, 2))
+            for j in range(2):
+                fill(GATE_O, g, j)
+            tt(GATE_F, g); pr(GATE_F, g)
+            for j in range(2, 2 + 1):
+                fill(GATE_O, g, j)
+            more(0)
+            if has(g - 1):
+                for s in slots(a - 4, 2):
+                    turn_back(GATE_O, s)
+            for j in range(2 + 1, 4):
+                fill(GATE_O, g, j)
+            if has(g - 1):
+                for s in slots(a - 4 + 2, 4 - 2):
+                    turn_back(GATE_O, s)
+                pr(GATE_O, g - 1)
+            sq(GATE_O, g)
+            sum_g(g, nc.gpsimd)
+            more(1)
+
+
+        sum_g(3, nc.vector)
+        each(tanh_cell, slots(12, 4))
+        tt(GATE_O, 3); pr(GATE_O, 3)

@@ -29,7 +29,10 @@ WORDS = WIDTH // 2
 W_X, W_H = 0, 1
 QUADS = 4
 PSUM_BANKS = 8
-LOADS = "u0a x h0a u0b h0b b K k u1a R u1b r u2 h1 h2 u3 c0 h3 c1 c2 c3"
+PAIR = 2
+N_PAIRS = SLOTS // PAIR
+PAIR_COLS = PAIR * WIDTH
+LOADS = "u0a x b h0a u0b h0b Ka k u1a Ra u1b r u2a h1a Kb Rb u2b h1b h2 u3 c0 h3 c1 c2 c3"
 
 FLOPS = 2 * WIDTH * GATES * WIDTH * (P + P * SLOTS)
 
@@ -46,10 +49,10 @@ def tile_rlstmcell_pb_kernel(
         loads = ctx.enter_context(tc.tile_pool(name="loads", bufs=1))
         stage = ctx.enter_context(tc.tile_pool(name="stage", bufs=3))
         gates = ctx.enter_context(tc.tile_pool(name="gates", bufs=12))
-        work = ctx.enter_context(tc.tile_pool(name="work", bufs=6))
-        longer = ctx.enter_context(tc.tile_pool(name="longer", bufs=8))
-        z_banks = ctx.enter_context(tc.psum_pool(name="z_banks", bufs=4))
-        t_banks = ctx.enter_context(tc.psum_pool(name="t_banks", bufs=4))
+        rows = ctx.enter_context(tc.tile_pool(name="rows", bufs=4))
+        outs = ctx.enter_context(tc.tile_pool(name="outs", bufs=6))
+        z_banks = ctx.enter_context(tc.psum_pool(name="z_banks", bufs=PSUM_BANKS // 2))
+        t_banks = ctx.enter_context(tc.psum_pool(name="t_banks", bufs=PSUM_BANKS // 2))
 
         ident = consts.tile([P, P], FP32)
         w_words = consts.tile([P, 2, 2 * GATES * WIDTH], U8, align_bytes=64)
@@ -104,10 +107,10 @@ def tile_rlstmcell_pb_kernel(
             elif kind == "b":
                 nc.sync.dma_start(out=bias_rows[0 : GATES * CHUNKS, :], in_=bias.rearrange("(j p) -> j p", p=P))
                 nc.sync.dma_start(out=bias_row0[0:1, :], in_=bias[GATE_I * WIDTH : (GATE_I + 1) * WIDTH].unsqueeze(0))
-            elif kind == "R":
-                nc.sync.dma_start(out=w_words[:, W_H, :].bitcast(I32), in_=recurrent_kernel_words[0].bitcast(I32))
-            elif kind == "K":
-                nc.sync.dma_start(out=w_words[:, W_X, :].bitcast(I32), in_=kernel_words[0].bitcast(I32))
+            elif kind in "KR":
+                w, source = (W_X, kernel_words) if kind == "K" else (W_H, recurrent_kernel_words)
+                a, b = {"": (0, 6 * WIDTH), "a": (0, 4 * WIDTH), "b": (4 * WIDTH, 6 * WIDTH)}[what[1:]]
+                nc.sync.dma_start(out=w_words[:, w, a:b].bitcast(I32), in_=source[0, :, a:b].bitcast(I32))
             elif kind == "r":
                 load_scales(W_H, recurrent_kernel_scales)
             elif kind == "k":
@@ -124,44 +127,42 @@ def tile_rlstmcell_pb_kernel(
         for what in LOADS.split():
             load_named(what)
 
-        cand = [consts.tile([P, WIDTH], FP32, name="cand%d" % s) for s in range(SLOTS)]
-        c_new, tanh_c, gate_i_of, z_of, T_of, grouped_of = {}, {}, {}, {}, {}, {}
-
         def slot_cols(s):
-            return slice((s % GROUP_SLOTS) * WIDTH, (s % GROUP_SLOTS + 1) * WIDTH)
+            return slice(s % GROUP_SLOTS * WIDTH, (s % GROUP_SLOTS + 1) * WIDTH)
 
-        def turn(rows, s, grouped):
-            bank = t_banks.tile([P, 2, P], FP32, tag="t_bank")
-            for u in range(2):
-                nc.tensor.transpose(bank[:, u, :], rows[:, s * WORDS + u : (s + 1) * WORDS : 2], ident[:])
-            return bank, grouped
+        def half(s):
+            return slice(s % PAIR * WIDTH, (s % PAIR + 1) * WIDTH)
 
-        def unturn(pair):
-            bank, grouped = pair
+        grouped_of, cand, gate_i, i_bank, z_of, T_of, back, c_new, tanh_c = {}, {}, {}, {}, {}, {}, {}, {}, {}
+        late = set()
+
+        def turn(source, first, n_slots, name):
+            bank = t_banks.tile([P, n_slots, 2, P], FP32, tag="t_bank")
+            for n in range(n_slots):
+                for u in range(2):
+                    nc.tensor.transpose(
+                        bank[:, n, u, :], source[:, (first + n) * WORDS + u : (first + n + 1) * WORDS : 2], ident[:]
+                    )
+            grouped_of[name] = bank
+
+        def group(name, n_slots, grouped):
             nc.vector.tensor_copy(
-                out=grouped[:].bitcast(FP32).rearrange("p (b u) -> p b u", b=P, u=2), in_=bank[:].rearrange("p u b -> p b u")
+                out=grouped[:].bitcast(FP32).rearrange("p (s b u) -> p s b u", s=n_slots, b=P, u=2),
+                in_=grouped_of[name][:].rearrange("p s u b -> p s b u"),
             )
+            grouped_of[name] = grouped
 
         def turn_h(p):
-            rows = h_sb[p // 2][:].bitcast(FP32)
-            bank = t_banks.tile([P, 2, 2, P], FP32, tag="t_bank")
-            for n in range(2):
-                s = 2 * (p % 2) + n
-                for u in range(2):
-                    nc.tensor.transpose(bank[:, n, u, :], rows[:, s * WORDS + u : (s + 1) * WORDS : 2], ident[:])
-            grouped_of[p] = bank
+            turn(h_sb[p // 2][:].bitcast(FP32), p % 2 * PAIR, PAIR, p)
 
-        def copy_h(p):
-            grouped = stage.tile([P, 2 * 4 * P], BF16, name="grouped", align_bytes=64)
-            nc.vector.tensor_copy(
-                out=grouped[:].bitcast(FP32).rearrange("p (s b u) -> p s b u", s=2, b=P, u=2), in_=grouped_of[p][:].rearrange("p s u b -> p s b u")
-            )
-            grouped_of[p] = grouped
+        def group_h(p):
+            grouped = stage.tile([P, PAIR * 4 * P], BF16, name="grouped", align_bytes=64)
+            group(p, PAIR, grouped)
 
         def quantise_h(p):
-            g, j = p // 2, p % 2
+            cols = slice(p % 2 * PAIR * P, (p % 2 + 1) * PAIR * P)
             nc.vector.quantize_mx(
-                out=h_codes[:, g, 2 * j * P : 2 * (j + 1) * P].bitcast(E4M3X4), scales=h_scales[:, g, 2 * j * P : 2 * (j + 1) * P], in_=grouped_of[p][:]
+                out=h_codes[:, p // 2, cols].bitcast(E4M3X4), scales=h_scales[:, p // 2, cols], in_=grouped_of[p][:]
             )
 
         def gate_words(w, gate):
@@ -170,52 +171,41 @@ def tile_rlstmcell_pb_kernel(
         def gate_scales(w, gate):
             return w_scales[:, w, WIDTH * gate : WIDTH * (gate + 1)]
 
-        def tanh_candidate(s, n=1):
-            for k in range(s, s + n):
-                nc.scalar.activation(out=cand[k][:], in_=u_sb[k // GROUP_SLOTS][:, slot_cols(k)], func=TANH)
+        def tanh_candidate(p):
+            cand[p] = consts.tile([P, PAIR_COLS], FP32, name="cand%d" % p)
+            cols = slice(p % 2 * PAIR_COLS, (p % 2 + 1) * PAIR_COLS)
+            nc.scalar.activation(out=cand[p][:], in_=u_sb[p // 2][:, cols], func=TANH)
 
-        i_bank = {}
-
-        def fill_i(s):
-            g, j = s // GROUP_SLOTS, s % GROUP_SLOTS
+        def lone_pass(lhsT, lhsT_scale, w, name):
             bank = t_banks.tile([P, WIDTH], FP32, tag="t_bank")
             nc.tensor.matmul_mx(
-                out=bank[:],
-                lhsT=h_codes[:, g, j * P : (j + 1) * P].bitcast(E4M3X4),
-                lhsT_scale=h_scales[:, g, j * P : (j + 1) * P],
-                rhs=gate_words(W_H, GATE_I),
-                rhs_scale=gate_scales(W_H, GATE_I),
-                start=True,
-                stop=True,
+                out=bank[:], lhsT=lhsT.bitcast(E4M3X4), lhsT_scale=lhsT_scale,
+                rhs=gate_words(w, GATE_I), rhs_scale=gate_scales(w, GATE_I), start=True, stop=True,
             )
-            i_bank[s] = bank
+            i_bank[name] = bank
+
+        def fill_i(s):
+            g, cols = s // GROUP_SLOTS, slice(s % GROUP_SLOTS * P, (s % GROUP_SLOTS + 1) * P)
+            lone_pass(h_codes[:, g, cols], h_scales[:, g, cols], W_H, s)
 
         def add_i(s):
-            gate_i = work.tile([P, WIDTH], FP32, name="gate_i")
-            nc.vector.tensor_tensor(out=gate_i[:], in0=i_bank[s][:], in1=x_part_i[:], op=ADD)
-            gate_i_of[s] = gate_i
+            if s % PAIR == 0:
+                gate_i[s // PAIR] = rows.tile([P, PAIR_COLS], FP32, name="gate_i")
+            nc.vector.tensor_tensor(out=gate_i[s // PAIR][:, half(s)], in0=i_bank[s][:], in1=x_part_i[:], op=ADD)
 
-        def squash_i(s):
-            nc.scalar.activation(out=gate_i_of[s][:], in_=gate_i_of[s][:], func=SIGMOID)
-
-        def times_candidate(s):
-            nc.gpsimd.tensor_tensor(out=cand[s][:], in0=gate_i_of[s][:], in1=cand[s][:], op=MULT)
+        def squash_i(p):
+            nc.scalar.activation(out=gate_i[p][:], in_=gate_i[p][:], func=SIGMOID)
+            for s in (PAIR * p, PAIR * p + 1):
+                nc.gpsimd.tensor_tensor(out=cand[p][:, half(s)], in0=gate_i[p][:, half(s)], in1=cand[p][:, half(s)], op=MULT)
 
         def fill(gate, g, j):
             chunk = gate * CHUNKS + j
             z_T = z_banks.tile([P, PASS_COLS], FP32, name="z_T")
-            for w, codes, scales in (
-                (W_X, x_codes[:], x_scales[:]),
-                (W_H, h_codes[:, g, :], h_scales[:, g, :]),
-            ):
+            for w, codes, scales in ((W_X, x_codes[:], x_scales[:]), (W_H, h_codes[:, g, :], h_scales[:, g, :])):
                 nc.tensor.matmul_mx(
-                    out=z_T[:],
-                    lhsT=w_words[:, w, 2 * P * chunk : 2 * P * (chunk + 1)].bitcast(E2M1X4),
-                    lhsT_scale=w_scales[:, w, P * chunk : P * (chunk + 1)],
-                    rhs=codes.bitcast(E4M3X4),
-                    rhs_scale=scales,
-                    start=(w == W_X),
-                    stop=(w == W_H),
+                    out=z_T[:], lhsT=w_words[:, w, 2 * P * chunk : 2 * P * (chunk + 1)].bitcast(E2M1X4),
+                    lhsT_scale=w_scales[:, w, P * chunk : P * (chunk + 1)], rhs=codes.bitcast(E4M3X4), rhs_scale=scales,
+                    start=(w == W_X), stop=(w == W_H),
                 )
             z_of[gate, g, j] = z_T
 
@@ -227,194 +217,139 @@ def tile_rlstmcell_pb_kernel(
             )
             T_of[gate, g, j] = squashed
 
-        back = {}
-        late = set()
-
         def turn_back(gate, s):
-            g, q = s // GROUP_SLOTS, s % GROUP_SLOTS
             bank = t_banks.tile([P, WIDTH], FP32, tag="t_bank")
+            q = s % GROUP_SLOTS
             for j in range(CHUNKS):
-                nc.tensor.transpose(bank[:, j * P : (j + 1) * P], T_of[gate, g, j][:, q * P : (q + 1) * P], ident[:])
+                nc.tensor.transpose(
+                    bank[:, j * P : (j + 1) * P], T_of[gate, s // GROUP_SLOTS, j][:, q * P : (q + 1) * P], ident[:]
+                )
             back[gate, s] = bank
 
-        def product(gate, s):
-            g = s // GROUP_SLOTS
-            if gate == GATE_F:
-                c_new[s] = longer.tile([P, WIDTH], FP32, name="c_new")
-                nc.vector.tensor_tensor(out=c_new[s][:], in0=back[gate, s][:], in1=c_sb[g][:, slot_cols(s)], op=MULT)
-            else:
-                h_new = work.tile([P, WIDTH], FP32, name="h_new")
-                width = WIDTH // 2 if s == SLOTS - 1 else WIDTH
-                for b in range(0, WIDTH, width):
-                    nc.vector.tensor_tensor(
-                        out=h_new[:, b : b + width], in0=back[gate, s][:, b : b + width], in1=tanh_c[s][:, b : b + width], op=MULT
-                    )
-                    nc.sync.dma_start(out=out_0[:, s * WIDTH + b : s * WIDTH + b + width], in_=h_new[:, b : b + width])
+        def product_f(s):
+            if s % PAIR == 0:
+                c_new[s // PAIR] = rows.tile([P, PAIR_COLS], FP32, name="c_new")
+            nc.vector.tensor_tensor(
+                out=c_new[s // PAIR][:, half(s)], in0=back[GATE_F, s][:], in1=c_sb[s // GROUP_SLOTS][:, slot_cols(s)], op=MULT
+            )
+
+        def store_c(s):
+            nc.sync.dma_start(out=out_1[:, s * WIDTH : (s + 1) * WIDTH], in_=c_new[s // PAIR][:, half(s)])
 
         def add_up(s, engine):
-            engine.tensor_tensor(out=c_new[s][:], in0=c_new[s][:], in1=cand[s][:], op=ADD)
+            there = c_new[s // PAIR][:, half(s)]
+            engine.tensor_tensor(out=there, in0=there, in1=cand[s // PAIR][:, half(s)], op=ADD)
             if engine is nc.vector:
-                nc.sync.dma_start(out=out_1[:, s * WIDTH : (s + 1) * WIDTH], in_=c_new[s][:])
+                store_c(s)
             else:
                 late.add(s)
 
-        def tanh_cell(s):
-            tanh_c[s] = longer.tile([P, WIDTH], FP32, name="tanh_c")
-            nc.scalar.activation(out=tanh_c[s][:], in_=c_new[s][:], func=TANH)
-            if s in late:
-                nc.sync.dma_start(out=out_1[:, s * WIDTH : (s + 1) * WIDTH], in_=c_new[s][:])
+        def tanh_cell(p):
+            tanh_c[p] = rows.tile([P, PAIR_COLS], FP32, name="tanh_c")
+            if p >= N_PAIRS - 2:
+                for q in range(PAIR):
+                    nc.scalar.activation(out=tanh_c[p][:, q * WIDTH : (q + 1) * WIDTH], in_=c_new[p][:, q * WIDTH : (q + 1) * WIDTH], func=TANH)
+            else:
+                nc.scalar.activation(out=tanh_c[p][:], in_=c_new[p][:], func=TANH)
+            for s in (PAIR * p, PAIR * p + 1):
+                if s in late:
+                    store_c(s)
 
+        def product_o(s):
+            h_new = outs.tile([P, WIDTH], FP32, name="h_new")
+            width = WIDTH // 2 if s == SLOTS - 1 else WIDTH
+            for a in range(0, WIDTH, width):
+                b = s % PAIR * WIDTH + a
+                nc.vector.tensor_tensor(
+                    out=h_new[:, a : a + width], in0=back[GATE_O, s][:, a : a + width], in1=tanh_c[s // PAIR][:, b : b + width], op=MULT
+                )
+                nc.sync.dma_start(out=out_0[:, s * WIDTH + a : s * WIDTH + a + width], in_=h_new[:, a : a + width])
 
-        def turn_x():
-            grouped_of["x"] = turn(x_sb[:].bitcast(FP32), 0, x_once)
-        def copy_x():
-            unturn(grouped_of["x"])
-        def quantise_x():
-            nc.vector.quantize_mx(out=x_codes1[:].bitcast(E4M3X4), scales=x_scales1[:], in_=x_once[:])
-        hold = {}
-        def bias_pe():
-            nc.vector.tensor_copy(out=bias_rows_f32[:], in_=bias_rows[:])
-            hold["b"] = t_banks.tile([P, P], FP32, name="bias_bank", tag="t_bank")
-            nc.tensor.transpose(hold["b"][:], bias_rows_f32[:], ident[:])
-            hold["s"] = t_banks.tile([P, WIDTH], FP32, name="spread_bank", tag="t_bank")
-            nc.tensor.matmul(out=hold["s"][:], lhsT=ones[:], rhs=bias_row0[:], start=True, stop=True)
-        def bias_v():
-            nc.vector.tensor_copy(out=bias_T[:], in_=hold["b"][:, 0 : GATES * CHUNKS])
-        def bias_a():
-            nc.vector.tensor_copy(out=bias_i[:], in_=hold["s"][:])
-        def x_pe():
-            hold["x"] = t_banks.tile([P, WIDTH], FP32, name="x_bank", tag="t_bank")
-            nc.tensor.matmul_mx(
-                out=hold["x"][:], lhsT=x_codes1[:].bitcast(E4M3X4), lhsT_scale=x_scales1[:],
-                rhs=gate_words(W_X, GATE_I), rhs_scale=gate_scales(W_X, GATE_I), start=True, stop=True,
-            )
-        def x_v():
-            nc.vector.tensor_tensor(out=x_part_i[:], in0=hold["x"][:], in1=bias_i[:], op=ADD)
-        def spread_x():
-            nc.vector.tensor_copy(
-                out=x_codes[:].bitcast(I32).rearrange("p (s b) -> p s b", s=GROUP_SLOTS),
-                in_=x_codes1[:].bitcast(I32).unsqueeze(1).to_broadcast([P, GROUP_SLOTS, P]),
-            )
-            nc.vector.tensor_copy(
-                out=x_scales[:].bitcast(I32).rearrange("p (s w) -> p s w", s=GROUP_SLOTS),
-                in_=x_scales1[:].bitcast(I32).unsqueeze(1).to_broadcast([P, GROUP_SLOTS, P // 4]),
-            )
-
-        def has(g):
-            return 0 <= g < N_GROUPS
-        def slots(a, n):
-            return [s for s in range(a, a + n) if 0 <= s < SLOTS]
-        def pairs(a, n):
-            return [p for p in range(a, a + n) if 0 <= p < SLOTS // 2]
-        def each(fn, what):
-            for w in what:
-                fn(w)
-        def both(a, b, what):
-            for w in what:
-                a(w)
-                b(w)
-        def zf(gate, g):
-            for j in range(CHUNKS):
-                fill(gate, g, j)
-        def sq(gate, g, j0=0, n=4):
-            for j in range(j0, j0 + n):
-                squash(gate, g, j)
-        def tt(gate, g):
-            for s in slots(4 * g, 4):
-                turn_back(gate, s)
-        def pr(gate, g):
-            for s in slots(4 * g, 4):
-                product(gate, s)
-        def si(s):
-            squash_i(s)
-            times_candidate(s)
-        def su(s):
-            add_up(s, nc.gpsimd if s % 2 == 1 else nc.vector)
-        def prsu(g):
-            a = 4 * g
-            product(GATE_F, a); product(GATE_F, a + 1)
-            su(a + 1); su(a)
-            product(GATE_F, a + 2); product(GATE_F, a + 3)
-            su(a + 3); su(a + 2)
-        def tu(s):
-            tanh_candidate(s)
-        def tc_(g):
-            for s in slots(4 * g, 4):
-                tanh_cell(s)
-
-
-        turn_x(); copy_x(); turn_h(0); turn_h(1); quantise_x(); copy_h(0); copy_h(1)
-        bias_pe(); spread_x(); quantise_h(0); quantise_h(1); x_pe(); bias_v(); bias_a(); x_v()
-        done = [0]
-        def more(n):
-            for s in slots(done[0], n):
-                tu(s)
-            done[0] += n
-        more(10)
-        def sum_g(g, engine):
-            for s in slots(4 * g, 4):
+        def sums(g, engine):
+            for s in range(GROUP_SLOTS * g, GROUP_SLOTS * (g + 1)):
                 if (engine is nc.gpsimd) == (s % 4 == 3 and s < 12):
                     add_up(s, engine)
-        def H(p):
-            for q in pairs(p, 1):
-                turn_h(q); copy_h(q); quantise_h(q)
-        def I(s):
-            for q in slots(s, 2):
-                fill_i(q)
-            for q in slots(s, 2):
-                add_i(q)
-        def SI(s):
-            each(si, slots(s, 2))
-        def TC(s):
-            if s >= 0:
-                tanh_cell(s)
-            else:
-                more(1)
-        H(2) if 0 else None
+
+        def each(step, first, n, end):
+            for k in range(first, min(first + n, end)):
+                step(k)
+
+        done = [0]
+
+        def more_candidates(n):
+            each(tanh_candidate, done[0], n, N_PAIRS)
+            done[0] += n
+
+        idle_bank = z_banks.tile([P, PASS_COLS], FP32, name="z_T")
+        for n in range(3):
+            nc.tensor.matmul(out=idle_bank[:], lhsT=ones[:], rhs=zeros[:], start=True, stop=True)
+        turn(x_sb[:].bitcast(FP32), 0, 1, "x")
+        group("x", 1, x_once)
+        turn_h(0)
+        nc.vector.tensor_copy(out=bias_rows_f32[:], in_=bias_rows[:])
+        bias_bank = t_banks.tile([P, P], FP32, tag="t_bank")
+        nc.tensor.transpose(bias_bank[:], bias_rows_f32[:], ident[:])
+        spread_bank = t_banks.tile([P, WIDTH], FP32, tag="t_bank")
+        nc.tensor.matmul(out=spread_bank[:], lhsT=ones[:], rhs=bias_row0[:], start=True, stop=True)
+        turn_h(1)
+        nc.vector.quantize_mx(out=x_codes1[:].bitcast(E4M3X4), scales=x_scales1[:], in_=x_once[:])
+        group_h(0)
+        group_h(1)
+
+        nc.vector.tensor_copy(
+            out=x_codes[:].bitcast(I32).rearrange("p (s b) -> p s b", s=GROUP_SLOTS),
+            in_=x_codes1[:].bitcast(I32).unsqueeze(1).to_broadcast([P, GROUP_SLOTS, P]),
+        )
+        nc.vector.tensor_copy(
+            out=x_scales[:].bitcast(I32).rearrange("p (s w) -> p s w", s=GROUP_SLOTS),
+            in_=x_scales1[:].bitcast(I32).unsqueeze(1).to_broadcast([P, GROUP_SLOTS, P // 4]),
+        )
+        quantise_h(0)
+        quantise_h(1)
+        lone_pass(x_codes1[:], x_scales1[:], W_X, "x")
+        nc.vector.tensor_copy(out=bias_T[:], in_=bias_bank[:, 0 : GATES * CHUNKS])
+        nc.vector.tensor_copy(out=bias_i[:], in_=spread_bank[:])
+        nc.vector.tensor_tensor(out=x_part_i[:], in0=i_bank["x"][:], in1=bias_i[:], op=ADD)
+        more_candidates(5 - done[0])
 
         for g in range(N_GROUPS):
-
-            a = 4 * g
+            a, p = GROUP_SLOTS * g, 2 * g
             fill(GATE_F, g, 0)
-            fill_i(a + 0)
-            fill_i(a + 1)
-            fill(GATE_F, g, 1)
-            fill(GATE_F, g, 2)
-            fill(GATE_F, g, 3)
-            fill_i(a + 2)
-            fill_i(a + 3)
-
-            each(add_i, slots(a, 2))
-            if has(g - 1):
-                sum_g(g - 1, nc.vector)
-            each(add_i, slots(a + 2, 2))
-            sq(GATE_F, g)
-            each(turn_h, pairs(2 * g + 2, 2)); each(copy_h, pairs(2 * g + 2, 2)); each(quantise_h, pairs(2 * g + 2, 2))
-            more(1)
-            for j in range(0, 4, 2):
-                each(si, slots(a + j, 2))
+            each(fill_i, a, 2, SLOTS)
+            for j in range(1, CHUNKS):
+                fill(GATE_F, g, j)
+            each(fill_i, a + 2, 2, SLOTS)
+            each(add_i, a, 2, SLOTS)
+            if g > 0:
+                sums(g - 1, nc.vector)
+            each(add_i, a + 2, 2, SLOTS)
+            for j in range(CHUNKS):
+                squash(GATE_F, g, j)
+            each(turn_h, p + 2, 2, N_PAIRS)
+            each(group_h, p + 2, 2, N_PAIRS)
+            each(quantise_h, p + 2, 2, N_PAIRS)
+            pass
+            for q in range(2):
+                squash_i(p + q)
                 if g > 0:
-                    each(tanh_cell, slots(a - 4 + j, 2))
+                    tanh_cell(p - 2 + q)
             for j in range(2):
                 fill(GATE_O, g, j)
-            tt(GATE_F, g); pr(GATE_F, g)
-            for j in range(2, 2 + 1):
+            each(lambda s: turn_back(GATE_F, s), a, GROUP_SLOTS, SLOTS)
+            each(product_f, a, GROUP_SLOTS, SLOTS)
+            for j in range(2, 3):
                 fill(GATE_O, g, j)
-            more(0)
-            if has(g - 1):
-                for s in slots(a - 4, 2):
-                    turn_back(GATE_O, s)
-            for j in range(2 + 1, 4):
-                fill(GATE_O, g, j)
-            if has(g - 1):
-                for s in slots(a - 4 + 2, 4 - 2):
-                    turn_back(GATE_O, s)
-                pr(GATE_O, g - 1)
-            sq(GATE_O, g)
-            sum_g(g, nc.gpsimd)
-            more(1)
-
-
-        sum_g(3, nc.vector)
-        each(tanh_cell, slots(12, 4))
-        tt(GATE_O, 3); pr(GATE_O, 3)
+            if g > 0:
+                each(lambda s: turn_back(GATE_O, s), a - 4, 2, SLOTS)
+            fill(GATE_O, g, 3)
+            if g > 0:
+                each(lambda s: turn_back(GATE_O, s), a - 2, 2, SLOTS)
+                each(product_o, a - 4, GROUP_SLOTS, SLOTS)
+            for j in range(CHUNKS):
+                squash(GATE_O, g, j)
+            sums(g, nc.gpsimd)
+            more_candidates(1)
+        sums(N_GROUPS - 1, nc.vector)
+        each(tanh_cell, N_PAIRS - 2, 2, N_PAIRS)
+        each(lambda s: turn_back(GATE_O, s), SLOTS - 4, 4, SLOTS)
+        each(product_o, SLOTS - 4, 4, SLOTS)

@@ -32,7 +32,7 @@ PSUM_BANKS = 8
 PAIR = 2
 N_PAIRS = SLOTS // PAIR
 PAIR_COLS = PAIR * WIDTH
-LOADS = "u0a x b h0a u0b h0b Ka k u1a Ra u1b r u2a h1a Kb Rb u2b h1b h2 u3 c0 h3 c1 c2 c3"
+LOADS = "u0a x h0a u0b h0b b u1a Ka k Ra u1b r u2a h1a Kb Rb u2b h1b h2 u3 c0 h3 c1 c2 c3"
 
 FLOPS = 2 * WIDTH * GATES * WIDTH * (P + P * SLOTS)
 
@@ -174,7 +174,8 @@ def tile_rlstmcell_pb_kernel(
         def tanh_candidate(p):
             cand[p] = consts.tile([P, PAIR_COLS], FP32, name="cand%d" % p)
             cols = slice(p % 2 * PAIR_COLS, (p % 2 + 1) * PAIR_COLS)
-            nc.scalar.activation(out=cand[p][:], in_=u_sb[p // 2][:, cols], func=TANH)
+            for q in range(PAIR):
+                nc.scalar.activation(out=cand[p][:, q * WIDTH : (q + 1) * WIDTH], in_=u_sb[p // 2][:, (p % 2 * 2 + q) * WIDTH : (p % 2 * 2 + q + 1) * WIDTH], func=TANH)
 
         def lone_pass(lhsT, lhsT_scale, w, name):
             bank = t_banks.tile([P, WIDTH], FP32, tag="t_bank")
@@ -194,7 +195,8 @@ def tile_rlstmcell_pb_kernel(
             nc.vector.tensor_tensor(out=gate_i[s // PAIR][:, half(s)], in0=i_bank[s][:], in1=x_part_i[:], op=ADD)
 
         def squash_i(p):
-            nc.scalar.activation(out=gate_i[p][:], in_=gate_i[p][:], func=SIGMOID)
+            for q in range(PAIR):
+                nc.scalar.activation(out=gate_i[p][:, q * WIDTH : (q + 1) * WIDTH], in_=gate_i[p][:, q * WIDTH : (q + 1) * WIDTH], func=SIGMOID)
             for s in (PAIR * p, PAIR * p + 1):
                 nc.gpsimd.tensor_tensor(out=cand[p][:, half(s)], in0=gate_i[p][:, half(s)], in1=cand[p][:, half(s)], op=MULT)
 
@@ -246,7 +248,7 @@ def tile_rlstmcell_pb_kernel(
 
         def tanh_cell(p):
             tanh_c[p] = rows.tile([P, PAIR_COLS], FP32, name="tanh_c")
-            if p >= N_PAIRS - 2:
+            if True:
                 for q in range(PAIR):
                     nc.scalar.activation(out=tanh_c[p][:, q * WIDTH : (q + 1) * WIDTH], in_=c_new[p][:, q * WIDTH : (q + 1) * WIDTH], func=TANH)
             else:
@@ -280,9 +282,6 @@ def tile_rlstmcell_pb_kernel(
             each(tanh_candidate, done[0], n, N_PAIRS)
             done[0] += n
 
-        idle_bank = z_banks.tile([P, PASS_COLS], FP32, name="z_T")
-        for n in range(3):
-            nc.tensor.matmul(out=idle_bank[:], lhsT=ones[:], rhs=zeros[:], start=True, stop=True)
         turn(x_sb[:].bitcast(FP32), 0, 1, "x")
         group("x", 1, x_once)
         turn_h(0)

@@ -32,7 +32,7 @@ PSUM_BANKS = 8
 PAIR = 2
 N_PAIRS = SLOTS // PAIR
 PAIR_COLS = PAIR * WIDTH
-LOADS = "u0a x h0a u0b h0b b u1a Ka k Ra u1b r u2a h1a Kb Rb u2b h1b h2 u3 c0 h3 c1 c2 c3"
+LOADS = "u0a x h0a u0b h0b b u1a Ka k Ra u1b r u2a h1 Kb Rb c0 u2b h2 c1 u3 h3 c2 c3"
 
 FLOPS = 2 * WIDTH * GATES * WIDTH * (P + P * SLOTS)
 
@@ -79,11 +79,11 @@ def tile_rlstmcell_pb_kernel(
         u_sb = [loads.tile([P, GROUP_COLS], BF16, name="u_sb%d" % g) for g in range(N_GROUPS)]
 
         nc.vector.memset(warm[:], 0.0)
+        nc.vector.memset(ones[:], 1.0)
+        nc.vector.memset(zeros[:], 0.0)
         nc.scalar.activation(out=warm[:], in_=warm[:], func=SIGMOID)
         nc.vector.memset(bias_rows[:], 0.0)
         nc.vector.memset(bias_row0[:], 0.0)
-        nc.vector.memset(ones[:], 1.0)
-        nc.vector.memset(zeros[:], 0.0)
         nc.vector.memset(w_scales[:].bitcast(I32), 0)
         nc.vector.memset(x_scales1[:].bitcast(I32), 0)
         make_identity(nc, ident[:])
@@ -282,15 +282,24 @@ def tile_rlstmcell_pb_kernel(
             each(tanh_candidate, done[0], n, N_PAIRS)
             done[0] += n
 
+        def keep_warm(bank, n):
+            for k in range(n):
+                nc.tensor.matmul(out=bank[:], lhsT=ones[:], rhs=zeros[:], start=True, stop=True)
+
+        idle_bank = z_banks.tile([P, PASS_COLS], FP32, name="z_T")
+        keep_warm(idle_bank, 4)
         turn(x_sb[:].bitcast(FP32), 0, 1, "x")
         group("x", 1, x_once)
+        keep_warm(idle_bank, 1)
         turn_h(0)
+        keep_warm(idle_bank, 2)
         nc.vector.tensor_copy(out=bias_rows_f32[:], in_=bias_rows[:])
         bias_bank = t_banks.tile([P, P], FP32, tag="t_bank")
         nc.tensor.transpose(bias_bank[:], bias_rows_f32[:], ident[:])
         spread_bank = t_banks.tile([P, WIDTH], FP32, tag="t_bank")
         nc.tensor.matmul(out=spread_bank[:], lhsT=ones[:], rhs=bias_row0[:], start=True, stop=True)
         turn_h(1)
+        keep_warm(idle_bank, 1)
         nc.vector.quantize_mx(out=x_codes1[:].bitcast(E4M3X4), scales=x_scales1[:], in_=x_once[:])
         group_h(0)
         group_h(1)

@@ -269,7 +269,7 @@ def tile_rlstmcell_pb_kernel(
 
         def sums(g, engine):
             for s in range(GROUP_SLOTS * g, GROUP_SLOTS * (g + 1)):
-                if (engine is nc.gpsimd) == (s % 4 == 3 and s < 12):
+                if (engine is nc.gpsimd) == (s % 4 == 0 and s < 12):
                     add_up(s, engine)
 
         def each(step, first, n, end):
@@ -341,17 +341,14 @@ def tile_rlstmcell_pb_kernel(
                 squash_i(p + q)
                 if g > 0:
                     tanh_cell(p - 2 + q)
-            for j in range(2):
-                fill(GATE_O, g, j)
+            fill(GATE_O, g, 0)
+            fill(GATE_O, g, 1)
             each(lambda s: turn_back(GATE_F, s), a, GROUP_SLOTS, SLOTS)
             each(product_f, a, GROUP_SLOTS, SLOTS)
-            for j in range(2, 3):
-                fill(GATE_O, g, j)
-            if g > 0:
-                each(lambda s: turn_back(GATE_O, s), a - 4, 2, SLOTS)
+            fill(GATE_O, g, 2)
             fill(GATE_O, g, 3)
             if g > 0:
-                each(lambda s: turn_back(GATE_O, s), a - 2, 2, SLOTS)
+                each(lambda s: turn_back(GATE_O, s), a - 4, 4, SLOTS)
                 each(product_o, a - 4, GROUP_SLOTS, SLOTS)
             for j in range(CHUNKS):
                 squash(GATE_O, g, j)

@@ -32,7 +32,7 @@ PSUM_BANKS = 8
 PAIR = 2
 N_PAIRS = SLOTS // PAIR
 PAIR_COLS = PAIR * WIDTH
-LOADS = "u0a x h0a u0b h0b b u1a Ka k Ra u1b r u2a h1 Kb Rb c0 u2b h2 c1 u3 h3 c2 c3"
+LOADS = "u0a x h0a u0b h0b b u1a Ka k u1b Ra r u2a h1 Kb Rb c0 u2b h2 c1 u3 h3 c2 c3"
 
 FLOPS = 2 * WIDTH * GATES * WIDTH * (P + P * SLOTS)
 
@@ -198,18 +198,27 @@ def tile_rlstmcell_pb_kernel(
             for q in range(PAIR):
                 nc.scalar.activation(out=gate_i[p][:, q * WIDTH : (q + 1) * WIDTH], in_=gate_i[p][:, q * WIDTH : (q + 1) * WIDTH], func=SIGMOID)
             for s in (PAIR * p, PAIR * p + 1):
-                nc.gpsimd.tensor_tensor(out=cand[p][:, half(s)], in0=gate_i[p][:, half(s)], in1=cand[p][:, half(s)], op=MULT)
+                engine = nc.vector if s == 0 else nc.gpsimd
+                engine.tensor_tensor(out=cand[p][:, half(s)], in0=gate_i[p][:, half(s)], in1=cand[p][:, half(s)], op=MULT)
+
+        def one_pass(gate, g, j, w):
+            chunk = gate * CHUNKS + j
+            codes, scales = (x_codes[:], x_scales[:]) if w == W_X else (h_codes[:, g, :], h_scales[:, g, :])
+            nc.tensor.matmul_mx(
+                out=z_of[gate, g, j][:], lhsT=w_words[:, w, 2 * P * chunk : 2 * P * (chunk + 1)].bitcast(E2M1X4),
+                lhsT_scale=w_scales[:, w, P * chunk : P * (chunk + 1)], rhs=codes.bitcast(E4M3X4), rhs_scale=scales,
+                start=(w == W_X), stop=(w == W_H),
+            )
+
+        def open_bank(gate, g, j):
+            z_T = z_banks.tile([P, PASS_COLS], FP32, name="z_T")
+            z_of[gate, g, j] = z_T
+            one_pass(gate, g, j, W_X)
 
         def fill(gate, g, j):
-            chunk = gate * CHUNKS + j
-            z_T = z_banks.tile([P, PASS_COLS], FP32, name="z_T")
-            for w, codes, scales in ((W_X, x_codes[:], x_scales[:]), (W_H, h_codes[:, g, :], h_scales[:, g, :])):
-                nc.tensor.matmul_mx(
-                    out=z_T[:], lhsT=w_words[:, w, 2 * P * chunk : 2 * P * (chunk + 1)].bitcast(E2M1X4),
-                    lhsT_scale=w_scales[:, w, P * chunk : P * (chunk + 1)], rhs=codes.bitcast(E4M3X4), rhs_scale=scales,
-                    start=(w == W_X), stop=(w == W_H),
-                )
-            z_of[gate, g, j] = z_T
+            if (gate, g, j) not in z_of:
+                open_bank(gate, g, j)
+            one_pass(gate, g, j, W_H)
 
         def squash(gate, g, j):
             chunk = gate * CHUNKS + j
@@ -302,8 +311,6 @@ def tile_rlstmcell_pb_kernel(
         keep_warm(idle_bank, 1)
         nc.vector.quantize_mx(out=x_codes1[:].bitcast(E4M3X4), scales=x_scales1[:], in_=x_once[:])
         group_h(0)
-        group_h(1)
-
         nc.vector.tensor_copy(
             out=x_codes[:].bitcast(I32).rearrange("p (s b) -> p s b", s=GROUP_SLOTS),
             in_=x_codes1[:].bitcast(I32).unsqueeze(1).to_broadcast([P, GROUP_SLOTS, P]),
@@ -312,9 +319,13 @@ def tile_rlstmcell_pb_kernel(
             out=x_scales[:].bitcast(I32).rearrange("p (s w) -> p s w", s=GROUP_SLOTS),
             in_=x_scales1[:].bitcast(I32).unsqueeze(1).to_broadcast([P, GROUP_SLOTS, P // 4]),
         )
+        group_h(1)
+
         quantise_h(0)
         quantise_h(1)
         lone_pass(x_codes1[:], x_scales1[:], W_X, "x")
+        for j in range(4):
+            open_bank(GATE_F, 0, j)
         nc.vector.tensor_copy(out=bias_T[:], in_=bias_bank[:, 0 : GATES * CHUNKS])
         nc.vector.tensor_copy(out=bias_i[:], in_=spread_bank[:])
         nc.vector.tensor_tensor(out=x_part_i[:], in0=i_bank["x"][:], in1=bias_i[:], op=ADD)
@@ -346,9 +357,11 @@ def tile_rlstmcell_pb_kernel(
             each(lambda s: turn_back(GATE_F, s), a, GROUP_SLOTS, SLOTS)
             each(product_f, a, GROUP_SLOTS, SLOTS)
             fill(GATE_O, g, 2)
+            if g > 0:
+                each(lambda s: turn_back(GATE_O, s), a - 4, 2, SLOTS)
             fill(GATE_O, g, 3)
             if g > 0:
-                each(lambda s: turn_back(GATE_O, s), a - 4, 4, SLOTS)
+                each(lambda s: turn_back(GATE_O, s), a - 2, 2, SLOTS)
                 each(product_o, a - 4, GROUP_SLOTS, SLOTS)
             for j in range(CHUNKS):
                 squash(GATE_O, g, j)

@@ -32,7 +32,7 @@ PSUM_BANKS = 8
 PAIR = 2
 N_PAIRS = SLOTS // PAIR
 PAIR_COLS = PAIR * WIDTH
-LOADS = "u0a x h0a u0b h0b b u1a Ka k u1b Ra r u2a h1 Kb Rb c0 u2b h2 c1 u3 h3 c2 c3"
+LOADS = "u0a x u0b h0a h0b b u1a Ka k u1b Ra r u2a h1 Kb Rb c0 u2b h2 c1 u3 h3 c2 c3"
 
 FLOPS = 2 * WIDTH * GATES * WIDTH * (P + P * SLOTS)
 
@@ -302,11 +302,6 @@ def tile_rlstmcell_pb_kernel(
         keep_warm(idle_bank, 1)
         turn_h(0)
         keep_warm(idle_bank, 2)
-        nc.vector.tensor_copy(out=bias_rows_f32[:], in_=bias_rows[:])
-        bias_bank = t_banks.tile([P, P], FP32, tag="t_bank")
-        nc.tensor.transpose(bias_bank[:], bias_rows_f32[:], ident[:])
-        spread_bank = t_banks.tile([P, WIDTH], FP32, tag="t_bank")
-        nc.tensor.matmul(out=spread_bank[:], lhsT=ones[:], rhs=bias_row0[:], start=True, stop=True)
         turn_h(1)
         keep_warm(idle_bank, 1)
         nc.vector.quantize_mx(out=x_codes1[:].bitcast(E4M3X4), scales=x_scales1[:], in_=x_once[:])
@@ -319,6 +314,11 @@ def tile_rlstmcell_pb_kernel(
             out=x_scales[:].bitcast(I32).rearrange("p (s w) -> p s w", s=GROUP_SLOTS),
             in_=x_scales1[:].bitcast(I32).unsqueeze(1).to_broadcast([P, GROUP_SLOTS, P // 4]),
         )
+        nc.vector.tensor_copy(out=bias_rows_f32[:], in_=bias_rows[:])
+        bias_bank = t_banks.tile([P, P], FP32, tag="t_bank")
+        nc.tensor.transpose(bias_bank[:], bias_rows_f32[:], ident[:])
+        spread_bank = t_banks.tile([P, WIDTH], FP32, tag="t_bank")
+        nc.tensor.matmul(out=spread_bank[:], lhsT=ones[:], rhs=bias_row0[:], start=True, stop=True)
         group_h(1)
 
         quantise_h(0)

from contextlib import ExitStack

import concourse.mybir as mybir
from concourse.masks import make_identity

FP32 = mybir.dt.float32
BF16 = mybir.dt.bfloat16
I32 = mybir.dt.int32
U32 = mybir.dt.uint32
U8 = mybir.dt.uint8
E4M3X4 = mybir.dt.float8_e4m3fn_x4
E2M1X4 = mybir.dt.float4_e2m1fn_x4
SIGMOID = mybir.ActivationFunctionType.Sigmoid
TANH = mybir.ActivationFunctionType.Tanh
MULT = mybir.AluOpType.mult
ADD = mybir.AluOpType.add

P = 128
SLOTS = 16
WIDTH = 512
GATES = 3
GATE_I, GATE_F, GATE_O = 0, 1, 2
CHUNKS = WIDTH // P
GROUP_SLOTS = 4
N_GROUPS = SLOTS // GROUP_SLOTS
GROUP_COLS = GROUP_SLOTS * WIDTH
PASS_COLS = GROUP_SLOTS * P
WORDS = WIDTH // 2
W_X, W_H = 0, 1
QUADS = 4
PSUM_BANKS = 8
PAIR = 2
N_PAIRS = SLOTS // PAIR
PAIR_COLS = PAIR * WIDTH
LOADS = "u0a x u0b h0a h0b b u1a Ka k u1b Ra r u2a h1 Kb Rb c0 u2b h2 c1 u3 h3 c2 c3"

FLOPS = 2 * WIDTH * GATES * WIDTH * (P + P * SLOTS)


def tile_rlstmcell_pb_kernel(
    tc, inputs, h_state, c_state, c_upd, kernel_words, kernel_scales, recurrent_kernel_words, recurrent_kernel_scales, bias, out_0, out_1,
):
    nc = tc.nc
    c_upd_rows = c_upd.rearrange("b s d -> b (s d)")

    with ExitStack() as ctx:
        ctx.enter_context(tc.manual_schedule())
        consts = ctx.enter_context(tc.tile_pool(name="consts", bufs=1))
        loads = ctx.enter_context(tc.tile_pool(name="loads", bufs=1))
        stage = ctx.enter_context(tc.tile_pool(name="stage", bufs=3))
        gates = ctx.enter_context(tc.tile_pool(name="gates", bufs=12))
        rows = ctx.enter_context(tc.tile_pool(name="rows", bufs=4))
        outs = ctx.enter_context(tc.tile_pool(name="outs", bufs=6))
        z_banks = ctx.enter_context(tc.psum_pool(name="z_banks", bufs=PSUM_BANKS // 2))
        t_banks = ctx.enter_context(tc.psum_pool(name="t_banks", bufs=PSUM_BANKS // 2))

        ident = consts.tile([P, P], FP32)
        w_words = consts.tile([P, 2, 2 * GATES * WIDTH], U8, align_bytes=64)
        w_scales = consts.tile([P, 2, GATES * WIDTH], U8, align_bytes=64)
        bias_rows = consts.tile([P, P], BF16)
        bias_rows_f32 = consts.tile([P, P], FP32)
        bias_T = consts.tile([P, GATES * CHUNKS], FP32)
        bias_i = consts.tile([P, WIDTH], FP32)
        x_part_i = consts.tile([P, WIDTH], FP32)
        bias_row0 = consts.tile([P, WIDTH], BF16)
        ones = consts.tile([P, P], BF16)
        zeros = consts.tile([P, WIDTH], BF16)
        warm = consts.tile([P, 1], FP32)
        x_sb = consts.tile([P, WIDTH], BF16)
        x_once = consts.tile([P, 4 * P], BF16, align_bytes=64)
        x_codes1 = consts.tile([P, P], U32, align_bytes=64)
        x_scales1 = consts.tile([P, P], U8, align_bytes=64)
        x_codes = consts.tile([P, PASS_COLS], U32, align_bytes=64)
        x_scales = consts.tile([P, PASS_COLS], U8, align_bytes=64)
        h_codes = consts.tile([P, N_GROUPS, PASS_COLS], U32, align_bytes=64)
        h_scales = consts.tile([P, N_GROUPS, PASS_COLS], U8, align_bytes=64)
        h_sb = [loads.tile([P, GROUP_COLS], BF16, name="h_sb%d" % g) for g in range(N_GROUPS)]
        c_sb = [loads.tile([P, GROUP_COLS], BF16, name="c_sb%d" % g) for g in range(N_GROUPS)]
        u_sb = [loads.tile([P, GROUP_COLS], BF16, name="u_sb%d" % g) for g in range(N_GROUPS)]

        nc.vector.memset(warm[:], 0.0)
        nc.vector.memset(ones[:], 1.0)
        nc.vector.memset(zeros[:], 0.0)
        nc.scalar.activation(out=warm[:], in_=warm[:], func=SIGMOID)
        nc.vector.memset(bias_rows[:], 0.0)
        nc.vector.memset(bias_row0[:], 0.0)
        nc.vector.memset(w_scales[:].bitcast(I32), 0)
        nc.vector.memset(x_scales1[:].bitcast(I32), 0)
        make_identity(nc, ident[:])

        def load(tiles, rows, g, first_slot=0, n_slots=GROUP_SLOTS):
            a = first_slot * WIDTH
            b = a + n_slots * WIDTH
            nc.sync.dma_start(out=tiles[g][:, a:b], in_=rows[:, g * GROUP_COLS + a : g * GROUP_COLS + b])

        def load_scales(w, scales):
            for quad in range(QUADS):
                nc.sync.dma_start(
                    out=w_scales[32 * quad : 32 * quad + 4, w, :].bitcast(I32),
                    in_=scales[0, 4 * quad : 4 * quad + 4, :].bitcast(I32),
                )

        def load_named(what):
            kind = what[0]
            if kind == "x":
                nc.sync.dma_start(out=x_sb[:], in_=inputs)
            elif kind == "b":
                nc.sync.dma_start(out=bias_rows[0 : GATES * CHUNKS, :], in_=bias.rearrange("(j p) -> j p", p=P))
                nc.sync.dma_start(out=bias_row0[0:1, :], in_=bias[GATE_I * WIDTH : (GATE_I + 1) * WIDTH].unsqueeze(0))
            elif kind in "KR":
                w, source = (W_X, kernel_words) if kind == "K" else (W_H, recurrent_kernel_words)
                a, b = {"": (0, 6 * WIDTH), "a": (0, 4 * WIDTH), "b": (4 * WIDTH, 6 * WIDTH)}[what[1:]]
                nc.sync.dma_start(out=w_words[:, w, a:b].bitcast(I32), in_=source[0, :, a:b].bitcast(I32))
            elif kind == "r":
                load_scales(W_H, recurrent_kernel_scales)
            elif kind == "k":
                load_scales(W_X, kernel_scales)
            else:
                tiles, rows = {"u": (u_sb, c_upd_rows), "h": (h_sb, h_state), "c": (c_sb, c_state)}[kind]
                g = int(what[1])
                if len(what) == 2:
                    load(tiles, rows, g)
                else:
                    load(tiles, rows, g, 2 * (what[2] == "b"), 2)


        for what in LOADS.split():
            load_named(what)

        def slot_cols(s):
            return slice(s % GROUP_SLOTS * WIDTH, (s % GROUP_SLOTS + 1) * WIDTH)

        def half(s):
            return slice(s % PAIR * WIDTH, (s % PAIR + 1) * WIDTH)

        grouped_of, cand, gate_i, i_bank, z_of, T_of, back, c_new, tanh_c = {}, {}, {}, {}, {}, {}, {}, {}, {}
        late = set()

        def turn(source, first, n_slots, name):
            bank = t_banks.tile([P, n_slots, 2, P], FP32, tag="t_bank")
            for n in range(n_slots):
                for u in range(2):
                    nc.tensor.transpose(
                        bank[:, n, u, :], source[:, (first + n) * WORDS + u : (first + n + 1) * WORDS : 2], ident[:]
                    )
            grouped_of[name] = bank

        def group(name, n_slots, grouped):
            nc.vector.tensor_copy(
                out=grouped[:].bitcast(FP32).rearrange("p (s b u) -> p s b u", s=n_slots, b=P, u=2),
                in_=grouped_of[name][:].rearrange("p s u b -> p s b u"),
            )
            grouped_of[name] = grouped

        def turn_h(p):
            turn(h_sb[p // 2][:].bitcast(FP32), p % 2 * PAIR, PAIR, p)

        def group_h(p):
            grouped = stage.tile([P, PAIR * 4 * P], BF16, name="grouped", align_bytes=64)
            group(p, PAIR, grouped)

        def quantise_h(p):
            cols = slice(p % 2 * PAIR * P, (p % 2 + 1) * PAIR * P)
            nc.vector.quantize_mx(
                out=h_codes[:, p // 2, cols].bitcast(E4M3X4), scales=h_scales[:, p // 2, cols], in_=grouped_of[p][:]
            )

        def gate_words(w, gate):
            return w_words[:, w, 2 * WIDTH * gate : 2 * WIDTH * (gate + 1)].bitcast(E2M1X4)

        def gate_scales(w, gate):
            return w_scales[:, w, WIDTH * gate : WIDTH * (gate + 1)]

        def tanh_candidate(p):
            cand[p] = consts.tile([P, PAIR_COLS], FP32, name="cand%d" % p)
            cols = slice(p % 2 * PAIR_COLS, (p % 2 + 1) * PAIR_COLS)
            for q in range(PAIR):
                nc.scalar.activation(out=cand[p][:, q * WIDTH : (q + 1) * WIDTH], in_=u_sb[p // 2][:, (p % 2 * 2 + q) * WIDTH : (p % 2 * 2 + q + 1) * WIDTH], func=TANH)

        def lone_pass(lhsT, lhsT_scale, w, name):
            bank = t_banks.tile([P, WIDTH], FP32, tag="t_bank")
            nc.tensor.matmul_mx(
                out=bank[:], lhsT=lhsT.bitcast(E4M3X4), lhsT_scale=lhsT_scale,
                rhs=gate_words(w, GATE_I), rhs_scale=gate_scales(w, GATE_I), start=True, stop=True,
            )
            i_bank[name] = bank

        def fill_i(s):
            g, cols = s // GROUP_SLOTS, slice(s % GROUP_SLOTS * P, (s % GROUP_SLOTS + 1) * P)
            lone_pass(h_codes[:, g, cols], h_scales[:, g, cols], W_H, s)

        def add_i(s):
            if s % PAIR == 0:
                gate_i[s // PAIR] = rows.tile([P, PAIR_COLS], FP32, name="gate_i")
            nc.vector.tensor_tensor(out=gate_i[s // PAIR][:, half(s)], in0=i_bank[s][:], in1=x_part_i[:], op=ADD)

        def squash_i(p):
            for q in range(PAIR):
                nc.scalar.activation(out=gate_i[p][:, q * WIDTH : (q + 1) * WIDTH], in_=gate_i[p][:, q * WIDTH : (q + 1) * WIDTH], func=SIGMOID)
            for s in (PAIR * p, PAIR * p + 1):
                engine = nc.vector if s == 0 else nc.gpsimd
                engine.tensor_tensor(out=cand[p][:, half(s)], in0=gate_i[p][:, half(s)], in1=cand[p][:, half(s)], op=MULT)

        def one_pass(gate, g, j, w):
            chunk = gate * CHUNKS + j
            codes, scales = (x_codes[:], x_scales[:]) if w == W_X else (h_codes[:, g, :], h_scales[:, g, :])
            nc.tensor.matmul_mx(
                out=z_of[gate, g, j][:], lhsT=w_words[:, w, 2 * P * chunk : 2 * P * (chunk + 1)].bitcast(E2M1X4),
                lhsT_scale=w_scales[:, w, P * chunk : P * (chunk + 1)], rhs=codes.bitcast(E4M3X4), rhs_scale=scales,
                start=(w == W_X), stop=(w == W_H),
            )

        def open_bank(gate, g, j):
            z_T = z_banks.tile([P, PASS_COLS], FP32, name="z_T")
            z_of[gate, g, j] = z_T
            one_pass(gate, g, j, W_X)

        def fill(gate, g, j):
            if (gate, g, j) not in z_of:
                open_bank(gate, g, j)
            one_pass(gate, g, j, W_H)

        def squash(gate, g, j):
            chunk = gate * CHUNKS + j
            squashed = gates.tile([P, PASS_COLS], FP32, name="squashed")
            nc.scalar.activation(
                out=squashed[:], in_=z_of[gate, g, j][:], func=SIGMOID, bias=bias_T[:, chunk : chunk + 1], scale=1.0
            )
            T_of[gate, g, j] = squashed

        def turn_back(gate, s):
            bank = t_banks.tile([P, WIDTH], FP32, tag="t_bank")
            q = s % GROUP_SLOTS
            for j in range(CHUNKS):
                nc.tensor.transpose(
                    bank[:, j * P : (j + 1) * P], T_of[gate, s // GROUP_SLOTS, j][:, q * P : (q + 1) * P], ident[:]
                )
            back[gate, s] = bank

        def product_f(s):
            if s % PAIR == 0:
                c_new[s // PAIR] = rows.tile([P, PAIR_COLS], FP32, name="c_new")
            nc.vector.tensor_tensor(
                out=c_new[s // PAIR][:, half(s)], in0=back[GATE_F, s][:], in1=c_sb[s // GROUP_SLOTS][:, slot_cols(s)], op=MULT
            )

        def store_c(s):
            nc.sync.dma_start(out=out_1[:, s * WIDTH : (s + 1) * WIDTH], in_=c_new[s // PAIR][:, half(s)])

        def add_up(s, engine):
            there = c_new[s // PAIR][:, half(s)]
            engine.tensor_tensor(out=there, in0=there, in1=cand[s // PAIR][:, half(s)], op=ADD)
            if engine is nc.vector:
                store_c(s)
            else:
                late.add(s)

        def tanh_cell(p):
            tanh_c[p] = rows.tile([P, PAIR_COLS], FP32, name="tanh_c")
            if True:
                for q in range(PAIR):
                    nc.scalar.activation(out=tanh_c[p][:, q * WIDTH : (q + 1) * WIDTH], in_=c_new[p][:, q * WIDTH : (q + 1) * WIDTH], func=TANH)
            else:
                nc.scalar.activation(out=tanh_c[p][:], in_=c_new[p][:], func=TANH)
            for s in (PAIR * p, PAIR * p + 1):
                if s in late:
                    store_c(s)

        def product_o(s):
            h_new = outs.tile([P, WIDTH], FP32, name="h_new")
            width = WIDTH // 2 if s == SLOTS - 1 else WIDTH
            for a in range(0, WIDTH, width):
                b = s % PAIR * WIDTH + a
                nc.vector.tensor_tensor(
                    out=h_new[:, a : a + width], in0=back[GATE_O, s][:, a : a + width], in1=tanh_c[s // PAIR][:, b : b + width], op=MULT
                )
                nc.sync.dma_start(out=out_0[:, s * WIDTH + a : s * WIDTH + a + width], in_=h_new[:, a : a + width])

        def sums(g, engine):
            for s in range(GROUP_SLOTS * g, GROUP_SLOTS * (g + 1)):
                if (engine is nc.gpsimd) == (s % 4 == 0 and s < 12):
                    add_up(s, engine)

        def each(step, first, n, end):
            for k in range(first, min(first + n, end)):
                step(k)

        done = [0]

        def more_candidates(n):
            each(tanh_candidate, done[0], n, N_PAIRS)
            done[0] += n

        def keep_warm(bank, n):
            for k in range(n):
                nc.tensor.matmul(out=bank[:], lhsT=ones[:], rhs=zeros[:], start=True, stop=True)

        idle_bank = z_banks.tile([P, PASS_COLS], FP32, name="z_T")
        keep_warm(idle_bank, 4)
        turn(x_sb[:].bitcast(FP32), 0, 1, "x")
        group("x", 1, x_once)
        keep_warm(idle_bank, 1)
        turn_h(0)
        keep_warm(idle_bank, 2)
        turn_h(1)
        keep_warm(idle_bank, 1)
        nc.vector.quantize_mx(out=x_codes1[:].bitcast(E4M3X4), scales=x_scales1[:], in_=x_once[:])
        group_h(0)
        nc.vector.tensor_copy(
            out=x_codes[:].bitcast(I32).rearrange("p (s b) -> p s b", s=GROUP_SLOTS),
            in_=x_codes1[:].bitcast(I32).unsqueeze(1).to_broadcast([P, GROUP_SLOTS, P]),
        )
        nc.vector.tensor_copy(
            out=x_scales[:].bitcast(I32).rearrange("p (s w) -> p s w", s=GROUP_SLOTS),
            in_=x_scales1[:].bitcast(I32).unsqueeze(1).to_broadcast([P, GROUP_SLOTS, P // 4]),
        )
        nc.vector.tensor_copy(out=bias_rows_f32[:], in_=bias_rows[:])
        bias_bank = t_banks.tile([P, P], FP32, tag="t_bank")
        nc.tensor.transpose(bias_bank[:], bias_rows_f32[:], ident[:])
        spread_bank = t_banks.tile([P, WIDTH], FP32, tag="t_bank")
        nc.tensor.matmul(out=spread_bank[:], lhsT=ones[:], rhs=bias_row0[:], start=True, stop=True)
        group_h(1)

        quantise_h(0)
        quantise_h(1)
        lone_pass(x_codes1[:], x_scales1[:], W_X, "x")
        for j in range(4):
            open_bank(GATE_F, 0, j)
        nc.vector.tensor_copy(out=bias_T[:], in_=bias_bank[:, 0 : GATES * CHUNKS])
        nc.vector.tensor_copy(out=bias_i[:], in_=spread_bank[:])
        nc.vector.tensor_tensor(out=x_part_i[:], in0=i_bank["x"][:], in1=bias_i[:], op=ADD)
        more_candidates(5 - done[0])

        for g in range(N_GROUPS):
            a, p = GROUP_SLOTS * g, 2 * g
            fill(GATE_F, g, 0)
            each(fill_i, a, 2, SLOTS)
            for j in range(1, CHUNKS):
                fill(GATE_F, g, j)
            each(fill_i, a + 2, 2, SLOTS)
            each(add_i, a, 2, SLOTS)
            if g > 0:
                sums(g - 1, nc.vector)
            each(add_i, a + 2, 2, SLOTS)
            for j in range(CHUNKS):
                squash(GATE_F, g, j)
            each(turn_h, p + 2, 2, N_PAIRS)
            each(group_h, p + 2, 2, N_PAIRS)
            each(quantise_h, p + 2, 2, N_PAIRS)
            pass
            for q in range(2):
                squash_i(p + q)
                if g > 0:
                    tanh_cell(p - 2 + q)
            fill(GATE_O, g, 0)
            fill(GATE_O, g, 1)
            each(lambda s: turn_back(GATE_F, s), a, GROUP_SLOTS, SLOTS)
            each(product_f, a, GROUP_SLOTS, SLOTS)
            fill(GATE_O, g, 2)
            if g > 0:
                each(lambda s: turn_back(GATE_O, s), a - 4, 2, SLOTS)
            fill(GATE_O, g, 3)
            if g > 0:
                each(lambda s: turn_back(GATE_O, s), a - 2, 2, SLOTS)
                each(product_o, a - 4, GROUP_SLOTS, SLOTS)
            for j in range(CHUNKS):
                squash(GATE_O, g, j)
            sums(g, nc.gpsimd)
            more_candidates(1)
        sums(N_GROUPS - 1, nc.vector)
        each(tanh_cell, N_PAIRS - 2, 2, N_PAIRS)
        each(lambda s: turn_back(GATE_O, s), SLOTS - 4, 4, SLOTS)
        each(product_o, SLOTS - 4, 4, SLOTS)
